import numpy as np
import ml_dtypes


def mxq(x, axis, fmt="e4m3"):
    dtype, down = {"e4m3": (ml_dtypes.float8_e4m3fn, 7), "e5m2": (ml_dtypes.float8_e5m2, 14)}[fmt]
    v = np.moveaxis(np.asarray(x, np.float32).astype(ml_dtypes.bfloat16).astype(np.float64), axis, -1)
    blocks = v.reshape(v.shape[:-1] + (-1, 32))
    amax = np.abs(blocks).max(-1, keepdims=True)
    byte = np.maximum(np.where(amax > 0, np.frexp(amax)[1] - 1 + 127, 0) - down, 1)
    scale = np.exp2(byte - 127.0)
    codes = (blocks / scale).astype(np.float32).astype(dtype).astype(np.float64)
    return np.moveaxis((codes * scale).reshape(v.shape), -1, axis)


WIDE = False


def mx_kscale(k):
    if not WIDE:
        return np.ones(k)
    levels = np.array([10, -10, 5, -5, 0])
    a = np.random.permutation(np.resize(levels, k // 512 * 4)).reshape(k // 512, 4)
    idx = np.arange(k)
    return np.exp2(a[idx // 512, idx % 128 // 32])


BF16 = ml_dtypes.bfloat16


def bf(x):
    return np.asarray(x, np.float32).astype(BF16)


def f64(x):
    return np.asarray(x).astype(np.float64)


N, BT, C, M, TD, F, NL = 256, 4, 1024, 512, 256, 512, 4
R = N * BT


def setup_inputs():
    t = mx_kscale(C)
    return {"body": bf(np.random.standard_normal((N, BT, C)) * t),
            "tokens": bf(np.random.standard_normal((M, C)) * 2.0 / t),
            "tfeat": bf(np.random.standard_normal((M, C)) * 2.0 * t),
            "Wf": bf(np.random.standard_normal((C, C)) / np.sqrt(C) * t[:, None] / t[None, :]),
            "b_f": bf(np.random.standard_normal(C) * 0.2 * t),
            "scale": bf(0.5 + 0.1 * np.random.standard_normal(1))}


def reference(body, tokens, tfeat, Wf, b_f, scale):
    xb = f64(body).reshape(R, C)
    s = xb @ f64(tokens).T * C ** -0.5
    e = np.exp(s - s.max(-1, keepdims=True))
    delta = (mxq(e, 1, "e4m3") @ mxq(f64(tfeat), 0, "e4m3")) / e.sum(-1, keepdims=True)
    u = delta + xb
    y = (mxq(u, 1, "e4m3") @ mxq(f64(Wf), 1, "e4m3").T) + f64(b_f)
    return (xb + y * f64(scale)).reshape(N, BT, C)

@@ -1,0 +1,316 @@
+from contextlib import ExitStack
+
+import concourse.mybir as mybir
+from concourse.masks import make_identity
+
+F32 = mybir.dt.float32
+BF16 = mybir.dt.bfloat16
+U32 = mybir.dt.uint32
+U8 = mybir.dt.uint8
+FP8X4 = mybir.dt.float8_e4m3fn_x4
+ALU = mybir.AluOpType
+ACT = mybir.ActivationFunctionType
+AXIS = mybir.AxisListType
+
+P = 128
+ROWS = 1024
+FEAT = 1024
+TOKENS = 512
+BANK = 512
+PACK = 4
+WORDS = FEAT // 2
+ROW_TILES = ROWS // P
+FEAT_BLOCKS = WORDS // P
+FEAT_PASSES = FEAT // (P * PACK)
+HALVES = FEAT // BANK
+SCORE_SCALE = FEAT ** -0.5
+SCORE_PASSES = FEAT // P
+
+PROJECT_LAG = 4
+W_TILES_PER_ROUND = 2
+
+FLOPS = 2 * ROWS * FEAT * TOKENS + 2 * ROWS * TOKENS * FEAT + 2 * ROWS * FEAT * FEAT
+
+
+def tile_reins_attention4_pa_kernel(tc, body, tokens, tfeat, Wf, b_f, scale, out):
+    nc = tc.nc
+    x_rows = body.flatten_outer_dims().rearrange("(p t) c -> p t c", t=ROW_TILES)
+    out_rows = out.flatten_outer_dims().rearrange("(p t) c -> p t c", t=ROW_TILES)
+
+    with ExitStack() as ctx:
+        ctx.enter_context(tc.manual_schedule())
+        keep = ctx.enter_context(tc.tile_pool(name="keep", bufs=1))
+        ring = ctx.enter_context(tc.tile_pool(name="ring", bufs=3))
+        banks = ctx.enter_context(tc.psum_pool(name="banks", bufs=8))
+
+        x_pairs = [keep.tile([P, 2, FEAT], BF16, name="x_pair%d" % j) for j in range(ROW_TILES // 2)]
+        w_pairs = [keep.tile([P, 2, FEAT], BF16, name="w_pair%d" % j) for j in range(FEAT // P // 2)]
+        tok_sb = keep.tile([P, TOKENS // P, FEAT], BF16, name="tok_sb")
+        tf_raw = keep.tile([P, PACK, FEAT], BF16, name="tf_raw")
+        tok_rows = tokens.rearrange("(a p) c -> p a c", p=P)
+        w_rows = Wf.rearrange("(a p) c -> p a c", p=P)
+
+        def load_x(j):
+            nc.sync.dma_start(out=x_pairs[j][:], in_=x_rows[:, 2 * j : 2 * j + 2, :])
+
+        def load_w(j):
+            nc.sync.dma_start(out=w_pairs[j][:], in_=w_rows[:, 2 * j : 2 * j + 2, :])
+
+        load_x(0)
+        for a in range(TOKENS // P):
+            nc.sync.dma_start(out=tok_sb[:, a, :], in_=tok_rows[:, a, :])
+        nc.sync.dma_start(
+            out=tf_raw[:].rearrange("q (h e) c -> q h (e c)", e=2),
+            in_=tfeat.rearrange("(h q e) c -> q h (e c)", h=2, e=2),
+        )
+        load_w(0)
+        load_w(1)
+        load_x(1)
+        load_w(2)
+        load_w(3)
+        load_x(2)
+        load_x(3)
+
+        def x_tile(t):
+            return x_pairs[t // 2][:, t % 2, :]
+
+        ident = keep.tile([P, P], F32, name="ident")
+        make_identity(nc, ident[:])
+        ones = keep.tile([P, P], BF16, name="ones")
+        nc.vector.memset(ones[:], 1.0)
+
+        SPARE = 32
+        row0 = keep.tile([P, FEAT + SPARE], BF16, name="row0")
+        nc.vector.memset(row0[:], 0.0)
+        nc.scalar.dma_start(out=row0[0:1, 0:FEAT], in_=b_f.unsqueeze(0))
+        nc.scalar.dma_start(out=row0[0:1, FEAT : FEAT + 1], in_=scale.unsqueeze(0))
+        scale_col = keep.tile([P, 1], F32, name="scale_col")
+        scaled_bias = keep.tile([P, FEAT], F32, name="scaled_bias")
+        residual = [keep.tile([P, FEAT], F32, name="residual%d" % t) for t in range(ROW_TILES)]
+
+        def prepare_residuals():
+            scale_bank = banks.tile([P, SPARE], F32, tag="bank", name="scale_bank")
+            nc.tensor.matmul(out=scale_bank[:], lhsT=ones[:], rhs=row0[:, FEAT:], start=True, stop=True)
+            nc.vector.tensor_copy(out=scale_col[:], in_=scale_bank[:, 0:1])
+            for h in range(HALVES):
+                cols = slice(h * BANK, (h + 1) * BANK)
+                bias_bank = banks.tile([P, BANK], F32, tag="bank", name="bias_bank")
+                nc.tensor.matmul(out=bias_bank[:], lhsT=ones[:], rhs=row0[:, cols], start=True, stop=True)
+                nc.vector.tensor_scalar(
+                    out=scaled_bias[:, cols], in0=bias_bank[:], scalar1=scale_col[:], scalar2=None, op0=ALU.mult
+                )
+            for t in range(ROW_TILES):
+                nc.gpsimd.tensor_tensor(out=residual[t][:], in0=x_tile(t), in1=scaled_bias[:], op=ALU.add)
+
+        def transpose_words(src_words, blocks, name):
+            bank = banks.tile([P, blocks, P], F32, tag="bank", name=name)
+            for blk in range(blocks):
+                nc.tensor.transpose(
+                    out=bank[:, blk, :], in_=src_words[:, blk * P : (blk + 1) * P], identity=ident[:]
+                )
+            return bank
+
+        def group_words(grouped, bank, passes):
+            nc.scalar.copy(
+                out=grouped[:].bitcast(F32).rearrange("q (g r h) -> q g r h", g=passes, h=2),
+                in_=bank[:].rearrange("q (g h) r -> q g r h", h=2),
+            )
+
+        tok_T = keep.tile([P, FEAT_BLOCKS, TOKENS], F32, name="tok_T")
+        x_T = {}
+
+        def x_transpose(t):
+            bank = transpose_words(x_tile(t).bitcast(F32), FEAT_BLOCKS, "x_bank")
+            x_T[t] = ring.tile([P, FEAT_BLOCKS, P], F32, name="x_T")
+            nc.scalar.copy(out=x_T[t][:], in_=bank[:])
+
+        x_transpose(0)
+        tok_banks = [banks.tile([P, TOKENS], F32, tag="bank", name="tok_bank%d" % blk) for blk in range(FEAT_BLOCKS)]
+        for a in range(TOKENS // P):
+            tok_words = tok_sb[:, a, :].bitcast(F32)
+            for blk in range(FEAT_BLOCKS):
+                nc.tensor.transpose(
+                    out=tok_banks[blk][:, a * P : (a + 1) * P],
+                    in_=tok_words[:, blk * P : (blk + 1) * P],
+                    identity=ident[:],
+                )
+        for blk in range(FEAT_BLOCKS):
+            if blk % 2 == 0:
+                nc.vector.tensor_copy(out=tok_T[:, blk, :], in_=tok_banks[blk][:])
+            else:
+                nc.scalar.copy(out=tok_T[:, blk, :], in_=tok_banks[blk][:])
+
+        row_max = keep.tile([P, ROW_TILES], F32, name="row_max")
+        exp_bias = keep.tile([P, ROW_TILES], F32, name="exp_bias")
+        e_sum = keep.tile([P, ROW_TILES], F32, name="e_sum")
+        e_sum_inv = keep.tile([P, ROW_TILES], F32, name="e_sum_inv")
+        e_rows = {}
+
+        def score_passes(t, bank, passes):
+            x_halves = x_T[t][:].bitcast(BF16).rearrange("q b (r e) -> q b r e", e=2)
+            tok_halves = tok_T[:].bitcast(BF16).rearrange("q b (m e) -> q b m e", e=2)
+            for k in passes:
+                nc.tensor.matmul(
+                    out=bank[:],
+                    lhsT=x_halves[:, k // 2, :, k % 2],
+                    rhs=tok_halves[:, k // 2, :, k % 2],
+                    start=(k == 0),
+                    stop=(k == SCORE_PASSES - 1),
+                )
+
+        def softmax_numerators(t, bank):
+            col = slice(t, t + 1)
+            nc.vector.tensor_reduce(out=row_max[:, col], in_=bank[:], axis=AXIS.X, op=ALU.max)
+            nc.vector.tensor_scalar(
+                out=exp_bias[:, col], in0=row_max[:, col], scalar1=-SCORE_SCALE, scalar2=None, op0=ALU.mult
+            )
+            e_rows[t] = ring.tile([P, TOKENS], BF16, name="e_rows")
+            nc.scalar.activation(
+                out=e_rows[t][:],
+                in_=bank[:],
+                func=ACT.Exp,
+                bias=exp_bias[:, col],
+                scale=SCORE_SCALE,
+                accum_out=e_sum[:, col],
+            )
+
+        tf_grouped = keep.tile([P, FEAT, PACK], BF16, name="tf_grouped", align_bytes=64)
+        tf_codes = keep.tile([P, FEAT], U32, name="tf_codes", align_bytes=64)
+        tf_scales = keep.tile([P, FEAT], U8, name="tf_scales", align_bytes=64)
+
+        def quantise_tfeat():
+            for h in range(HALVES):
+                cols = slice(h * BANK, (h + 1) * BANK)
+                nc.vector.tensor_copy(
+                    out=tf_grouped[:, cols, :].rearrange("q (c i) j -> q c j i", i=4),
+                    in_=tf_raw[:, :, cols].rearrange("q j (c i) -> q c j i", i=4),
+                )
+            for h in range(HALVES):
+                cols = slice(h * BANK, (h + 1) * BANK)
+                nc.vector.quantize_mx(
+                    out=tf_codes[:, cols].bitcast(FP8X4),
+                    scales=tf_scales[:, cols],
+                    in_=tf_grouped[:, cols, :].rearrange("q c j -> q (c j)"),
+                )
+
+        e_codes = {}
+        e_scales = {}
+        u_rows = {}
+
+        def e_transpose(t):
+            bank = transpose_words(e_rows[t][:].bitcast(F32), TOKENS // 2 // P, "e_bank")
+            e_grouped = ring.tile([P, P * PACK], BF16, name="e_grouped", align_bytes=64)
+            group_words(e_grouped, bank, 1)
+            e_codes[t] = ring.tile([P, P], U32, name="e_codes", align_bytes=64)
+            e_scales[t] = ring.tile([P, P], U8, name="e_scales", align_bytes=64)
+            nc.vector.quantize_mx(out=e_codes[t][:].bitcast(FP8X4), scales=e_scales[t][:], in_=e_grouped[:])
+
+        def attend(t):
+            col = slice(t, t + 1)
+            nc.vector.reciprocal(out=e_sum_inv[:, col], in_=e_sum[:, col])
+            u_rows[t] = ring.tile([P, FEAT], BF16, name="u_rows")
+            for h in range(HALVES):
+                cols = slice(h * BANK, (h + 1) * BANK)
+                bank = banks.tile([P, BANK], F32, tag="bank", name="delta_bank")
+                nc.tensor.matmul_mx(
+                    out=bank[:],
+                    lhsT=e_codes[t][:].bitcast(FP8X4),
+                    lhsT_scale=e_scales[t][:],
+                    rhs=tf_codes[:, cols].bitcast(FP8X4),
+                    rhs_scale=tf_scales[:, cols],
+                    start=True,
+                    stop=True,
+                )
+                nc.vector.scalar_tensor_tensor(
+                    out=u_rows[t][:, cols],
+                    in0=bank[:],
+                    scalar=e_sum_inv[:, col],
+                    in1=x_tile(t)[:, cols],
+                    op0=ALU.mult,
+                    op1=ALU.add,
+                )
+
+        w_codes = keep.tile([P, FEAT_PASSES, FEAT], U32, name="w_codes", align_bytes=64)
+        w_scales = keep.tile([P, FEAT_PASSES, FEAT], U8, name="w_scales", align_bytes=64)
+        w_grouped = {}
+        u_codes = [keep.tile([P, FEAT_PASSES, P], U32, name="u_codes%d" % t, align_bytes=64) for t in range(ROW_TILES)]
+        u_scales = [keep.tile([P, FEAT_PASSES, P], U8, name="u_scales%d" % t, align_bytes=64) for t in range(ROW_TILES)]
+
+        def w_transpose(a):
+            bank = transpose_words(w_pairs[a // 2][:, a % 2, :].bitcast(F32), FEAT_BLOCKS, "w_bank")
+            w_grouped[a] = ring.tile([P, FEAT], BF16, name="w_grouped", bufs=2 * W_TILES_PER_ROUND, align_bytes=64)
+            group_words(w_grouped[a], bank, FEAT_PASSES)
+
+        def w_quantise(a):
+            rows = slice(a * P, (a + 1) * P)
+            for g in range(FEAT_PASSES):
+                nc.vector.quantize_mx(
+                    out=w_codes[:, g, rows].bitcast(FP8X4),
+                    scales=w_scales[:, g, rows],
+                    in_=w_grouped[a][:, g * P * PACK : (g + 1) * P * PACK],
+                )
+
+        def u_transpose(t):
+            bank = transpose_words(u_rows[t][:].bitcast(F32), FEAT_BLOCKS, "u_bank")
+            u_grouped = ring.tile([P, FEAT], BF16, name="u_grouped", align_bytes=64)
+            group_words(u_grouped, bank, FEAT_PASSES)
+            nc.vector.quantize_mx(
+                out=u_codes[t][:].rearrange("q g r -> q (g r)").bitcast(FP8X4),
+                scales=u_scales[t][:].rearrange("q g r -> q (g r)"),
+                in_=u_grouped[:],
+            )
+
+        def project(t):
+            for h in range(HALVES):
+                cols = slice(h * BANK, (h + 1) * BANK)
+                bank = banks.tile([P, BANK], F32, tag="bank", name="y_bank")
+                for g in range(FEAT_PASSES):
+                    nc.tensor.matmul_mx(
+                        out=bank[:],
+                        lhsT=u_codes[t][:, g, :].bitcast(FP8X4),
+                        lhsT_scale=u_scales[t][:, g, :],
+                        rhs=w_codes[:, g, cols].bitcast(FP8X4),
+                        rhs_scale=w_scales[:, g, cols],
+                        start=(g == 0),
+                        stop=(g == FEAT_PASSES - 1),
+                    )
+                result = ring.tile([P, BANK], F32, name="result", bufs=4)
+                nc.vector.scalar_tensor_tensor(
+                    out=result[:],
+                    in0=bank[:],
+                    scalar=scale_col[:],
+                    in1=residual[t][:, cols],
+                    op0=ALU.mult,
+                    op1=ALU.add,
+                )
+                nc.sync.dma_start(out=out_rows[:, t, cols], in_=result[:])
+
+        def is_tile(t):
+            return 0 <= t < ROW_TILES
+
+        for i in range(ROW_TILES + PROJECT_LAG):
+            for a in range((i - 1) * W_TILES_PER_ROUND, i * W_TILES_PER_ROUND):
+                if 0 <= a < FEAT // P:
+                    w_quantise(a)
+            if is_tile(i - PROJECT_LAG):
+                project(i - PROJECT_LAG)
+            if is_tile(i):
+                score_bank = banks.tile([P, TOKENS], F32, tag="bank", name="score_bank")
+                score_passes(i, score_bank, range(0, SCORE_PASSES // 2))
+            if is_tile(i - 1):
+                e_transpose(i - 1)
+            if is_tile(i - 2):
+                u_transpose(i - 2)
+            if is_tile(i + 1):
+                x_transpose(i + 1)
+            if is_tile(i):
+                score_passes(i, score_bank, range(SCORE_PASSES // 2, SCORE_PASSES))
+                softmax_numerators(i, score_bank)
+            if i == 0:
+                prepare_residuals()
+                quantise_tfeat()
+            for a in range(i * W_TILES_PER_ROUND, (i + 1) * W_TILES_PER_ROUND):
+                if a < FEAT // P:
+                    w_transpose(a)
+            if is_tile(i - 1):
+                attend(i - 1)

@@ -88,7 +88,7 @@ def tile_reins_attention4_pa_kernel(tc, body, tokens, tfeat, Wf, b_f, scale, out
         scaled_bias = keep.tile([P, FEAT], F32, name="scaled_bias")
         residual = [keep.tile([P, FEAT], F32, name="residual%d" % t) for t in range(ROW_TILES)]
 
-        def prepare_residuals():
+        def spread_bias():
             scale_bank = banks.tile([P, SPARE], F32, tag="bank", name="scale_bank")
             nc.tensor.matmul(out=scale_bank[:], lhsT=ones[:], rhs=row0[:, FEAT:], start=True, stop=True)
             nc.vector.tensor_copy(out=scale_col[:], in_=scale_bank[:, 0:1])
@@ -99,8 +99,9 @@ def tile_reins_attention4_pa_kernel(tc, body, tokens, tfeat, Wf, b_f, scale, out
                 nc.vector.tensor_scalar(
                     out=scaled_bias[:, cols], in0=bias_bank[:], scalar1=scale_col[:], scalar2=None, op0=ALU.mult
                 )
-            for t in range(ROW_TILES):
-                nc.gpsimd.tensor_tensor(out=residual[t][:], in0=x_tile(t), in1=scaled_bias[:], op=ALU.add)
+
+        def make_residual(t):
+            nc.vector.tensor_tensor(out=residual[t][:], in0=x_tile(t), in1=scaled_bias[:], op=ALU.add)
 
         def transpose_words(src_words, blocks, name):
             bank = banks.tile([P, blocks, P], F32, tag="bank", name=name)
@@ -307,8 +308,10 @@ def tile_reins_attention4_pa_kernel(tc, body, tokens, tfeat, Wf, b_f, scale, out
                 score_passes(i, score_bank, range(SCORE_PASSES // 2, SCORE_PASSES))
                 softmax_numerators(i, score_bank)
             if i == 0:
-                prepare_residuals()
+                spread_bias()
                 quantise_tfeat()
+            if is_tile(i):
+                make_residual(i)
             for a in range(i * W_TILES_PER_ROUND, (i + 1) * W_TILES_PER_ROUND):
                 if a < FEAT // P:
                     w_transpose(a)

@@ -26,8 +26,14 @@ HALVES = FEAT // BANK
 SCORE_SCALE = FEAT ** -0.5
 SCORE_PASSES = FEAT // P
 
-PROJECT_LAG = 4
-W_TILES_PER_ROUND = 2
+X_LEAD = 2
+E_LAG = 1
+ATTEND_LAG = 2
+U_LAG = 4
+SCORE_ROUNDS = ROW_TILES
+PROJECTS_PER_ROUND = 2
+ROUNDS = SCORE_ROUNDS + ROW_TILES // PROJECTS_PER_ROUND
+RIDERS = 2
 
 FLOPS = 2 * ROWS * FEAT * TOKENS + 2 * ROWS * TOKENS * FEAT + 2 * ROWS * FEAT * FEAT
 
@@ -56,23 +62,25 @@ def tile_reins_attention4_pa_kernel(tc, body, tokens, tfeat, Wf, b_f, scale, out
         def load_w(j):
             nc.sync.dma_start(out=w_pairs[j][:], in_=w_rows[:, 2 * j : 2 * j + 2, :])
 
-        load_x(0)
         for a in range(TOKENS // P):
             nc.sync.dma_start(out=tok_sb[:, a, :], in_=tok_rows[:, a, :])
+        load_x(0)
+        load_w(0)
+        load_x(1)
         nc.sync.dma_start(
             out=tf_raw[:].rearrange("q (h e) c -> q h (e c)", e=2),
             in_=tfeat.rearrange("(h q e) c -> q h (e c)", h=2, e=2),
         )
-        load_w(0)
-        load_w(1)
-        load_x(1)
-        load_w(2)
-        load_w(3)
-        load_x(2)
-        load_x(3)
+        for j in range(1, ROW_TILES // 2):
+            load_w(j)
+            if j + 1 < ROW_TILES // 2:
+                load_x(j + 1)
 
         def x_tile(t):
             return x_pairs[t // 2][:, t % 2, :]
+
+        def w_tile(a):
+            return w_pairs[a // 2][:, a % 2, :]
 
         ident = keep.tile([P, P], F32, name="ident")
         make_identity(nc, ident[:])
@@ -88,7 +96,7 @@ def tile_reins_attention4_pa_kernel(tc, body, tokens, tfeat, Wf, b_f, scale, out
         scaled_bias = keep.tile([P, FEAT], F32, name="scaled_bias")
         residual = [keep.tile([P, FEAT], F32, name="residual%d" % t) for t in range(ROW_TILES)]
 
-        def spread_bias():
+        def prepare_residuals():
             scale_bank = banks.tile([P, SPARE], F32, tag="bank", name="scale_bank")
             nc.tensor.matmul(out=scale_bank[:], lhsT=ones[:], rhs=row0[:, FEAT:], start=True, stop=True)
             nc.vector.tensor_copy(out=scale_col[:], in_=scale_bank[:, 0:1])
@@ -99,17 +107,18 @@ def tile_reins_attention4_pa_kernel(tc, body, tokens, tfeat, Wf, b_f, scale, out
                 nc.vector.tensor_scalar(
                     out=scaled_bias[:, cols], in0=bias_bank[:], scalar1=scale_col[:], scalar2=None, op0=ALU.mult
                 )
+            for t in range(ROW_TILES):
+                nc.gpsimd.tensor_tensor(out=residual[t][:], in0=x_tile(t), in1=scaled_bias[:], op=ALU.add)
 
-        def make_residual(t):
-            nc.vector.tensor_tensor(out=residual[t][:], in0=x_tile(t), in1=scaled_bias[:], op=ALU.add)
+        def turn_bank(blocks, name):
+            return banks.tile([P, blocks, P], F32, tag="bank", name=name)
 
-        def transpose_words(src_words, blocks, name):
-            bank = banks.tile([P, blocks, P], F32, tag="bank", name=name)
-            for blk in range(blocks):
-                nc.tensor.transpose(
-                    out=bank[:, blk, :], in_=src_words[:, blk * P : (blk + 1) * P], identity=ident[:]
-                )
-            return bank
+        def turns_into(bank, rows_bf16, blocks):
+            words = rows_bf16.bitcast(F32)
+            return [(bank[:, b, :], words[:, b * P : (b + 1) * P]) for b in range(blocks)]
+
+        def turn(dst, src):
+            nc.tensor.transpose(out=dst, in_=src, identity=ident[:])
 
         def group_words(grouped, bank, passes):
             nc.scalar.copy(
@@ -120,51 +129,46 @@ def tile_reins_attention4_pa_kernel(tc, body, tokens, tfeat, Wf, b_f, scale, out
         tok_T = keep.tile([P, FEAT_BLOCKS, TOKENS], F32, name="tok_T")
         x_T = {}
 
-        def x_transpose(t):
-            bank = transpose_words(x_tile(t).bitcast(F32), FEAT_BLOCKS, "x_bank")
-            x_T[t] = ring.tile([P, FEAT_BLOCKS, P], F32, name="x_T")
-            nc.scalar.copy(out=x_T[t][:], in_=bank[:])
-
-        x_transpose(0)
-        tok_banks = [banks.tile([P, TOKENS], F32, tag="bank", name="tok_bank%d" % blk) for blk in range(FEAT_BLOCKS)]
+        tok_banks = [banks.tile([P, TOKENS], F32, tag="bank", name="tok_bank%d" % b) for b in range(FEAT_BLOCKS)]
         for a in range(TOKENS // P):
             tok_words = tok_sb[:, a, :].bitcast(F32)
-            for blk in range(FEAT_BLOCKS):
-                nc.tensor.transpose(
-                    out=tok_banks[blk][:, a * P : (a + 1) * P],
-                    in_=tok_words[:, blk * P : (blk + 1) * P],
-                    identity=ident[:],
-                )
-        for blk in range(FEAT_BLOCKS):
-            if blk % 2 == 0:
-                nc.vector.tensor_copy(out=tok_T[:, blk, :], in_=tok_banks[blk][:])
+            for b in range(FEAT_BLOCKS):
+                turn(tok_banks[b][:, a * P : (a + 1) * P], tok_words[:, b * P : (b + 1) * P])
+        for b in range(FEAT_BLOCKS):
+            if b % 2 == 0:
+                nc.vector.tensor_copy(out=tok_T[:, b, :], in_=tok_banks[b][:])
             else:
-                nc.scalar.copy(out=tok_T[:, blk, :], in_=tok_banks[blk][:])
+                nc.scalar.copy(out=tok_T[:, b, :], in_=tok_banks[b][:])
+        for t in range(X_LEAD):
+            x_bank = turn_bank(FEAT_BLOCKS, "x_bank")
+            for dst, src in turns_into(x_bank, x_tile(t), FEAT_BLOCKS):
+                turn(dst, src)
+            x_T[t] = ring.tile([P, FEAT_BLOCKS, P], F32, name="x_T", bufs=X_LEAD + 2)
+            if t % 2 == 0:
+                nc.vector.tensor_copy(out=x_T[t][:], in_=x_bank[:])
+            else:
+                nc.scalar.copy(out=x_T[t][:], in_=x_bank[:])
 
         row_max = keep.tile([P, ROW_TILES], F32, name="row_max")
         exp_bias = keep.tile([P, ROW_TILES], F32, name="exp_bias")
         e_sum = keep.tile([P, ROW_TILES], F32, name="e_sum")
         e_sum_inv = keep.tile([P, ROW_TILES], F32, name="e_sum_inv")
         e_rows = {}
+        tok_halves = tok_T[:].bitcast(BF16).rearrange("q b (m e) -> q b m e", e=2)
 
-        def score_passes(t, bank, passes):
+        def score_pass(t, bank, k):
             x_halves = x_T[t][:].bitcast(BF16).rearrange("q b (r e) -> q b r e", e=2)
-            tok_halves = tok_T[:].bitcast(BF16).rearrange("q b (m e) -> q b m e", e=2)
-            for k in passes:
-                nc.tensor.matmul(
-                    out=bank[:],
-                    lhsT=x_halves[:, k // 2, :, k % 2],
-                    rhs=tok_halves[:, k // 2, :, k % 2],
-                    start=(k == 0),
-                    stop=(k == SCORE_PASSES - 1),
-                )
+            nc.tensor.matmul(
+                out=bank[:],
+                lhsT=x_halves[:, k // 2, :, k % 2],
+                rhs=tok_halves[:, k // 2, :, k % 2],
+                start=(k == 0),
+                stop=(k == SCORE_PASSES - 1),
+            )
 
         def softmax_numerators(t, bank):
             col = slice(t, t + 1)
-            nc.vector.tensor_reduce(out=row_max[:, col], in_=bank[:], axis=AXIS.X, op=ALU.max)
-            nc.vector.tensor_scalar(
-                out=exp_bias[:, col], in0=row_max[:, col], scalar1=-SCORE_SCALE, scalar2=None, op0=ALU.mult
-            )
+            nc.scalar.mul(out=exp_bias[:, col], in_=row_max[:, col], mul=-SCORE_SCALE)
             e_rows[t] = ring.tile([P, TOKENS], BF16, name="e_rows")
             nc.scalar.activation(
                 out=e_rows[t][:],
@@ -198,18 +202,10 @@ def tile_reins_attention4_pa_kernel(tc, body, tokens, tfeat, Wf, b_f, scale, out
         e_scales = {}
         u_rows = {}
 
-        def e_transpose(t):
-            bank = transpose_words(e_rows[t][:].bitcast(F32), TOKENS // 2 // P, "e_bank")
-            e_grouped = ring.tile([P, P * PACK], BF16, name="e_grouped", align_bytes=64)
-            group_words(e_grouped, bank, 1)
-            e_codes[t] = ring.tile([P, P], U32, name="e_codes", align_bytes=64)
-            e_scales[t] = ring.tile([P, P], U8, name="e_scales", align_bytes=64)
-            nc.vector.quantize_mx(out=e_codes[t][:].bitcast(FP8X4), scales=e_scales[t][:], in_=e_grouped[:])
-
         def attend(t):
             col = slice(t, t + 1)
             nc.vector.reciprocal(out=e_sum_inv[:, col], in_=e_sum[:, col])
-            u_rows[t] = ring.tile([P, FEAT], BF16, name="u_rows")
+            u_rows[t] = ring.tile([P, FEAT], BF16, name="u_rows", bufs=U_LAG - ATTEND_LAG + 2)
             for h in range(HALVES):
                 cols = slice(h * BANK, (h + 1) * BANK)
                 bank = banks.tile([P, BANK], F32, tag="bank", name="delta_bank")
@@ -237,11 +233,6 @@ def tile_reins_attention4_pa_kernel(tc, body, tokens, tfeat, Wf, b_f, scale, out
         u_codes = [keep.tile([P, FEAT_PASSES, P], U32, name="u_codes%d" % t, align_bytes=64) for t in range(ROW_TILES)]
         u_scales = [keep.tile([P, FEAT_PASSES, P], U8, name="u_scales%d" % t, align_bytes=64) for t in range(ROW_TILES)]
 
-        def w_transpose(a):
-            bank = transpose_words(w_pairs[a // 2][:, a % 2, :].bitcast(F32), FEAT_BLOCKS, "w_bank")
-            w_grouped[a] = ring.tile([P, FEAT], BF16, name="w_grouped", bufs=2 * W_TILES_PER_ROUND, align_bytes=64)
-            group_words(w_grouped[a], bank, FEAT_PASSES)
-
         def w_quantise(a):
             rows = slice(a * P, (a + 1) * P)
             for g in range(FEAT_PASSES):
@@ -250,16 +241,6 @@ def tile_reins_attention4_pa_kernel(tc, body, tokens, tfeat, Wf, b_f, scale, out
                     scales=w_scales[:, g, rows],
                     in_=w_grouped[a][:, g * P * PACK : (g + 1) * P * PACK],
                 )
-
-        def u_transpose(t):
-            bank = transpose_words(u_rows[t][:].bitcast(F32), FEAT_BLOCKS, "u_bank")
-            u_grouped = ring.tile([P, FEAT], BF16, name="u_grouped", align_bytes=64)
-            group_words(u_grouped, bank, FEAT_PASSES)
-            nc.vector.quantize_mx(
-                out=u_codes[t][:].rearrange("q g r -> q (g r)").bitcast(FP8X4),
-                scales=u_scales[t][:].rearrange("q g r -> q (g r)"),
-                in_=u_grouped[:],
-            )
 
         def project(t):
             for h in range(HALVES):
@@ -289,31 +270,71 @@ def tile_reins_attention4_pa_kernel(tc, body, tokens, tfeat, Wf, b_f, scale, out
         def is_tile(t):
             return 0 <= t < ROW_TILES
 
-        for i in range(ROW_TILES + PROJECT_LAG):
-            for a in range((i - 1) * W_TILES_PER_ROUND, i * W_TILES_PER_ROUND):
-                if 0 <= a < FEAT // P:
-                    w_quantise(a)
-            if is_tile(i - PROJECT_LAG):
-                project(i - PROJECT_LAG)
+        for i in range(ROUNDS):
+            x_t, w_a, u_t, e_t = i + X_LEAD, i, i - U_LAG, i - E_LAG
+            if is_tile(w_a - 1):
+                w_quantise(w_a - 1)
+
+            turns = []
+            if is_tile(x_t):
+                x_bank = turn_bank(FEAT_BLOCKS, "x_bank")
+                turns.extend(turns_into(x_bank, x_tile(x_t), FEAT_BLOCKS))
+            if is_tile(w_a):
+                w_bank = turn_bank(FEAT_BLOCKS, "w_bank")
+                turns.extend(turns_into(w_bank, w_tile(w_a), FEAT_BLOCKS))
+            if is_tile(u_t):
+                u_bank = turn_bank(FEAT_BLOCKS, "u_bank")
+                turns.extend(turns_into(u_bank, u_rows[u_t][:], FEAT_BLOCKS))
+            if is_tile(e_t):
+                e_bank = turn_bank(TOKENS // 2 // P, "e_bank")
+                turns.extend(turns_into(e_bank, e_rows[e_t][:], TOKENS // 2 // P))
             if is_tile(i):
+                first_place = RIDERS * SCORE_PASSES - len(turns)
+                assert first_place >= 0
                 score_bank = banks.tile([P, TOKENS], F32, tag="bank", name="score_bank")
-                score_passes(i, score_bank, range(0, SCORE_PASSES // 2))
-            if is_tile(i - 1):
-                e_transpose(i - 1)
-            if is_tile(i - 2):
-                u_transpose(i - 2)
-            if is_tile(i + 1):
-                x_transpose(i + 1)
-            if is_tile(i):
-                score_passes(i, score_bank, range(SCORE_PASSES // 2, SCORE_PASSES))
-                softmax_numerators(i, score_bank)
+                for k in range(SCORE_PASSES):
+                    score_pass(i, score_bank, k)
+                    for place in range(max(k * RIDERS, first_place), (k + 1) * RIDERS):
+                        turn(*turns[place - first_place])
+                nc.vector.tensor_reduce(out=row_max[:, i : i + 1], in_=score_bank[:], axis=AXIS.X, op=ALU.max)
+            else:
+                for dst, src in turns:
+                    turn(dst, src)
             if i == 0:
-                spread_bias()
-                quantise_tfeat()
+                prepare_residuals()
+
+            if is_tile(x_t):
+                x_T[x_t] = ring.tile([P, FEAT_BLOCKS, P], F32, name="x_T", bufs=X_LEAD + 2)
+                nc.scalar.copy(out=x_T[x_t][:], in_=x_bank[:])
+            if is_tile(w_a):
+                w_grouped[w_a] = ring.tile([P, FEAT], BF16, name="w_grouped", align_bytes=64)
+                group_words(w_grouped[w_a], w_bank, FEAT_PASSES)
+            if is_tile(u_t):
+                u_grouped = ring.tile([P, FEAT], BF16, name="u_grouped", align_bytes=64)
+                group_words(u_grouped, u_bank, FEAT_PASSES)
+            if is_tile(e_t):
+                e_grouped = ring.tile([P, P * PACK], BF16, name="e_grouped", align_bytes=64)
+                group_words(e_grouped, e_bank, 1)
             if is_tile(i):
-                make_residual(i)
-            for a in range(i * W_TILES_PER_ROUND, (i + 1) * W_TILES_PER_ROUND):
-                if a < FEAT // P:
-                    w_transpose(a)
-            if is_tile(i - 1):
-                attend(i - 1)
+                softmax_numerators(i, score_bank)
+
+            if i == 1:
+                quantise_tfeat()
+            if is_tile(u_t):
+                nc.vector.quantize_mx(
+                    out=u_codes[u_t][:].rearrange("q g r -> q (g r)").bitcast(FP8X4),
+                    scales=u_scales[u_t][:].rearrange("q g r -> q (g r)"),
+                    in_=u_grouped[:],
+                )
+            if is_tile(e_t):
+                e_codes[e_t] = ring.tile([P, P], U32, name="e_codes", align_bytes=64)
+                e_scales[e_t] = ring.tile([P, P], U8, name="e_scales", align_bytes=64)
+                nc.vector.quantize_mx(
+                    out=e_codes[e_t][:].bitcast(FP8X4), scales=e_scales[e_t][:], in_=e_grouped[:]
+                )
+
+            if is_tile(i - ATTEND_LAG):
+                attend(i - ATTEND_LAG)
+            if i >= SCORE_ROUNDS:
+                for j in range(PROJECTS_PER_ROUND):
+                    project((i - SCORE_ROUNDS) * PROJECTS_PER_ROUND + j)

@@ -30,9 +30,10 @@ X_LEAD = 2
 E_LAG = 1
 ATTEND_LAG = 2
 U_LAG = 4
-SCORE_ROUNDS = ROW_TILES
-PROJECTS_PER_ROUND = 2
-ROUNDS = SCORE_ROUNDS + ROW_TILES // PROJECTS_PER_ROUND
+PROJECT_LAG = 6
+ROUNDS = ROW_TILES + PROJECT_LAG
+W_TILES = FEAT // P
+W_TILES_PER_ROUND = 2
 RIDERS = 2
 
 FLOPS = 2 * ROWS * FEAT * TOKENS + 2 * ROWS * TOKENS * FEAT + 2 * ROWS * FEAT * FEAT
@@ -67,14 +68,15 @@ def tile_reins_attention4_pa_kernel(tc, body, tokens, tfeat, Wf, b_f, scale, out
         load_x(0)
         load_w(0)
         load_x(1)
+        load_w(1)
         nc.sync.dma_start(
             out=tf_raw[:].rearrange("q (h e) c -> q h (e c)", e=2),
             in_=tfeat.rearrange("(h q e) c -> q h (e c)", h=2, e=2),
         )
-        for j in range(1, ROW_TILES // 2):
-            load_w(j)
-            if j + 1 < ROW_TILES // 2:
-                load_x(j + 1)
+        load_w(2)
+        load_x(2)
+        load_w(3)
+        load_x(3)
 
         def x_tile(t):
             return x_pairs[t // 2][:, t % 2, :]
@@ -242,46 +244,64 @@ def tile_reins_attention4_pa_kernel(tc, body, tokens, tfeat, Wf, b_f, scale, out
                     in_=w_grouped[a][:, g * P * PACK : (g + 1) * P * PACK],
                 )
 
-        def project(t):
-            for h in range(HALVES):
-                cols = slice(h * BANK, (h + 1) * BANK)
-                bank = banks.tile([P, BANK], F32, tag="bank", name="y_bank")
-                for g in range(FEAT_PASSES):
-                    nc.tensor.matmul_mx(
-                        out=bank[:],
-                        lhsT=u_codes[t][:, g, :].bitcast(FP8X4),
-                        lhsT_scale=u_scales[t][:, g, :],
-                        rhs=w_codes[:, g, cols].bitcast(FP8X4),
-                        rhs_scale=w_scales[:, g, cols],
-                        start=(g == 0),
-                        stop=(g == FEAT_PASSES - 1),
-                    )
-                result = ring.tile([P, BANK], F32, name="result", bufs=4)
-                nc.vector.scalar_tensor_tensor(
-                    out=result[:],
-                    in0=bank[:],
-                    scalar=scale_col[:],
-                    in1=residual[t][:, cols],
-                    op0=ALU.mult,
-                    op1=ALU.add,
+        def project_passes(t, h):
+            cols = slice(h * BANK, (h + 1) * BANK)
+            bank = banks.tile([P, BANK], F32, tag="bank", name="y_bank")
+            for g in range(FEAT_PASSES):
+                nc.tensor.matmul_mx(
+                    out=bank[:],
+                    lhsT=u_codes[t][:, g, :].bitcast(FP8X4),
+                    lhsT_scale=u_scales[t][:, g, :],
+                    rhs=w_codes[:, g, cols].bitcast(FP8X4),
+                    rhs_scale=w_scales[:, g, cols],
+                    start=(g == 0),
+                    stop=(g == FEAT_PASSES - 1),
                 )
-                nc.sync.dma_start(out=out_rows[:, t, cols], in_=result[:])
+            return bank
+
+        def finish_on_vector(t, h, bank):
+            cols = slice(h * BANK, (h + 1) * BANK)
+            result = ring.tile([P, BANK], F32, name="result", bufs=4)
+            nc.vector.scalar_tensor_tensor(
+                out=result[:], in0=bank[:], scalar=scale_col[:], in1=residual[t][:, cols], op0=ALU.mult, op1=ALU.add
+            )
+            nc.sync.dma_start(out=out_rows[:, t, cols], in_=result[:])
+
+        def finish_beside_vector(t, h, bank):
+            cols = slice(h * BANK, (h + 1) * BANK)
+            scaled = ring.tile([P, BANK], F32, name="scaled")
+            nc.scalar.activation(out=scaled[:], in_=bank[:], func=ACT.Copy, scale=scale_col[:])
+            result = ring.tile([P, BANK], F32, name="result_beside")
+            nc.gpsimd.tensor_tensor(out=result[:], in0=scaled[:], in1=residual[t][:, cols], op=ALU.add)
+            nc.sync.dma_start(out=out_rows[:, t, cols], in_=result[:])
+
+        def project(t):
+            first_bank = project_passes(t, 0)
+            second_bank = project_passes(t, 1)
+            if t == ROW_TILES - 1:
+                finish_on_vector(t, 0, first_bank)
+                finish_on_vector(t, 1, second_bank)
+            else:
+                finish_on_vector(t, 1, second_bank)
+                finish_beside_vector(t, 0, first_bank)
 
         def is_tile(t):
             return 0 <= t < ROW_TILES
 
         for i in range(ROUNDS):
-            x_t, w_a, u_t, e_t = i + X_LEAD, i, i - U_LAG, i - E_LAG
-            if is_tile(w_a - 1):
-                w_quantise(w_a - 1)
+            x_t, u_t, e_t = i + X_LEAD, i - U_LAG, i - E_LAG
+            w_now = [a for a in range(i * W_TILES_PER_ROUND, (i + 1) * W_TILES_PER_ROUND) if a < W_TILES]
+            for a in range((i - 1) * W_TILES_PER_ROUND, i * W_TILES_PER_ROUND):
+                if 0 <= a < W_TILES:
+                    w_quantise(a)
 
             turns = []
+            w_banks = [turn_bank(FEAT_BLOCKS, "w_bank") for a in w_now]
+            for a, w_bank in zip(w_now, w_banks):
+                turns.extend(turns_into(w_bank, w_tile(a), FEAT_BLOCKS))
             if is_tile(x_t):
                 x_bank = turn_bank(FEAT_BLOCKS, "x_bank")
                 turns.extend(turns_into(x_bank, x_tile(x_t), FEAT_BLOCKS))
-            if is_tile(w_a):
-                w_bank = turn_bank(FEAT_BLOCKS, "w_bank")
-                turns.extend(turns_into(w_bank, w_tile(w_a), FEAT_BLOCKS))
             if is_tile(u_t):
                 u_bank = turn_bank(FEAT_BLOCKS, "u_bank")
                 turns.extend(turns_into(u_bank, u_rows[u_t][:], FEAT_BLOCKS))
@@ -303,12 +323,12 @@ def tile_reins_attention4_pa_kernel(tc, body, tokens, tfeat, Wf, b_f, scale, out
             if i == 0:
                 prepare_residuals()
 
+            for a, w_bank in zip(w_now, w_banks):
+                w_grouped[a] = ring.tile([P, FEAT], BF16, name="w_grouped", bufs=2 * W_TILES_PER_ROUND, align_bytes=64)
+                group_words(w_grouped[a], w_bank, FEAT_PASSES)
             if is_tile(x_t):
                 x_T[x_t] = ring.tile([P, FEAT_BLOCKS, P], F32, name="x_T", bufs=X_LEAD + 2)
                 nc.scalar.copy(out=x_T[x_t][:], in_=x_bank[:])
-            if is_tile(w_a):
-                w_grouped[w_a] = ring.tile([P, FEAT], BF16, name="w_grouped", align_bytes=64)
-                group_words(w_grouped[w_a], w_bank, FEAT_PASSES)
             if is_tile(u_t):
                 u_grouped = ring.tile([P, FEAT], BF16, name="u_grouped", align_bytes=64)
                 group_words(u_grouped, u_bank, FEAT_PASSES)
@@ -335,6 +355,5 @@ def tile_reins_attention4_pa_kernel(tc, body, tokens, tfeat, Wf, b_f, scale, out
 
             if is_tile(i - ATTEND_LAG):
                 attend(i - ATTEND_LAG)
-            if i >= SCORE_ROUNDS:
-                for j in range(PROJECTS_PER_ROUND):
-                    project((i - SCORE_ROUNDS) * PROJECTS_PER_ROUND + j)
+            if is_tile(i - PROJECT_LAG):
+                project(i - PROJECT_LAG)

@@ -63,9 +63,10 @@ def tile_reins_attention4_pa_kernel(tc, body, tokens, tfeat, Wf, b_f, scale, out
         def load_w(j):
             nc.sync.dma_start(out=w_pairs[j][:], in_=w_rows[:, 2 * j : 2 * j + 2, :])
 
+        nc.sync.dma_start(out=x_pairs[0][:, 0, :], in_=x_rows[:, 0, :])
         for a in range(TOKENS // P):
             nc.sync.dma_start(out=tok_sb[:, a, :], in_=tok_rows[:, a, :])
-        load_x(0)
+        nc.sync.dma_start(out=x_pairs[0][:, 1, :], in_=x_rows[:, 1, :])
         load_w(0)
         load_x(1)
         load_w(1)
@@ -128,20 +129,10 @@ def tile_reins_attention4_pa_kernel(tc, body, tokens, tfeat, Wf, b_f, scale, out
                 in_=bank[:].rearrange("q (g h) r -> q g r h", h=2),
             )
 
-        tok_T = keep.tile([P, FEAT_BLOCKS, TOKENS], F32, name="tok_T")
+        tok_T = keep.tile([P, FEAT_BLOCKS, 2, TOKENS], BF16, name="tok_T")
         x_T = {}
 
-        tok_banks = [banks.tile([P, TOKENS], F32, tag="bank", name="tok_bank%d" % b) for b in range(FEAT_BLOCKS)]
-        for a in range(TOKENS // P):
-            tok_words = tok_sb[:, a, :].bitcast(F32)
-            for b in range(FEAT_BLOCKS):
-                turn(tok_banks[b][:, a * P : (a + 1) * P], tok_words[:, b * P : (b + 1) * P])
-        for b in range(FEAT_BLOCKS):
-            if b % 2 == 0:
-                nc.vector.tensor_copy(out=tok_T[:, b, :], in_=tok_banks[b][:])
-            else:
-                nc.scalar.copy(out=tok_T[:, b, :], in_=tok_banks[b][:])
-        for t in range(X_LEAD):
+        def turn_x_early(t):
             x_bank = turn_bank(FEAT_BLOCKS, "x_bank")
             for dst, src in turns_into(x_bank, x_tile(t), FEAT_BLOCKS):
                 turn(dst, src)
@@ -151,19 +142,34 @@ def tile_reins_attention4_pa_kernel(tc, body, tokens, tfeat, Wf, b_f, scale, out
             else:
                 nc.scalar.copy(out=x_T[t][:], in_=x_bank[:])
 
+        turn_x_early(0)
+        tok_banks = [banks.tile([P, TOKENS], F32, tag="bank", name="tok_bank%d" % b) for b in range(FEAT_BLOCKS)]
+        for a in range(TOKENS // P):
+            tok_words = tok_sb[:, a, :].bitcast(F32)
+            for b in range(FEAT_BLOCKS):
+                turn(tok_banks[b][:, a * P : (a + 1) * P], tok_words[:, b * P : (b + 1) * P])
+        for b in range(FEAT_BLOCKS):
+            for e in range(2):
+                halves = tok_banks[b][:].bitcast(BF16).rearrange("q (m e) -> q e m", e=2)
+                if b % 2 == 0:
+                    nc.vector.tensor_copy(out=tok_T[:, b, e, :], in_=halves[:, e, :])
+                else:
+                    nc.scalar.copy(out=tok_T[:, b, e, :], in_=halves[:, e, :])
+        turn_x_early(1)
+
         row_max = keep.tile([P, ROW_TILES], F32, name="row_max")
         exp_bias = keep.tile([P, ROW_TILES], F32, name="exp_bias")
         e_sum = keep.tile([P, ROW_TILES], F32, name="e_sum")
         e_sum_inv = keep.tile([P, ROW_TILES], F32, name="e_sum_inv")
         e_rows = {}
-        tok_halves = tok_T[:].bitcast(BF16).rearrange("q b (m e) -> q b m e", e=2)
 
         def score_pass(t, bank, k):
+            block, e = 2 * (k // 4) + k % 2, k % 4 // 2
             x_halves = x_T[t][:].bitcast(BF16).rearrange("q b (r e) -> q b r e", e=2)
             nc.tensor.matmul(
                 out=bank[:],
-                lhsT=x_halves[:, k // 2, :, k % 2],
-                rhs=tok_halves[:, k // 2, :, k % 2],
+                lhsT=x_halves[:, block, :, e],
+                rhs=tok_T[:, block, e, :],
                 start=(k == 0),
                 stop=(k == SCORE_PASSES - 1),
             )

@@ -33,7 +33,10 @@ U_LAG = 4
 PROJECT_LAG = 6
 ROUNDS = ROW_TILES + PROJECT_LAG
 W_TILES = FEAT // P
-W_TILES_PER_ROUND = 2
+W_TILES_PER_HALF = W_TILES // HALVES
+W_ROUNDS = ((0,), (1, 2), (3, 4), (5, 6), (7,))
+W_QUANTISE_ROUNDS = (3, 5)
+WARM_MATMULS = 4
 RIDERS = 2
 
 FLOPS = 2 * ROWS * FEAT * TOKENS + 2 * ROWS * TOKENS * FEAT + 2 * ROWS * FEAT * FEAT
@@ -67,17 +70,17 @@ def tile_reins_attention4_pa_kernel(tc, body, tokens, tfeat, Wf, b_f, scale, out
         for a in range(TOKENS // P):
             nc.sync.dma_start(out=tok_sb[:, a, :], in_=tok_rows[:, a, :])
         nc.sync.dma_start(out=x_pairs[0][:, 1, :], in_=x_rows[:, 1, :])
-        load_w(0)
         load_x(1)
-        load_w(1)
+        load_w(0)
         nc.sync.dma_start(
             out=tf_raw[:].rearrange("q (h e) c -> q h (e c)", e=2),
             in_=tfeat.rearrange("(h q e) c -> q h (e c)", h=2, e=2),
         )
-        load_w(2)
         load_x(2)
-        load_w(3)
+        load_w(1)
+        load_w(2)
         load_x(3)
+        load_w(3)
 
         def x_tile(t):
             return x_pairs[t // 2][:, t % 2, :]
@@ -87,31 +90,36 @@ def tile_reins_attention4_pa_kernel(tc, body, tokens, tfeat, Wf, b_f, scale, out
 
         ident = keep.tile([P, P], F32, name="ident")
         make_identity(nc, ident[:])
-        ones = keep.tile([P, P], BF16, name="ones")
+        ones = keep.tile([P, BANK], BF16, name="ones")
         nc.vector.memset(ones[:], 1.0)
 
         SPARE = 32
         row0 = keep.tile([P, FEAT + SPARE], BF16, name="row0")
-        nc.vector.memset(row0[:], 0.0)
+        nc.vector.memset(row0[:].bitcast(U32), 0)
         nc.scalar.dma_start(out=row0[0:1, 0:FEAT], in_=b_f.unsqueeze(0))
         nc.scalar.dma_start(out=row0[0:1, FEAT : FEAT + 1], in_=scale.unsqueeze(0))
         scale_col = keep.tile([P, 1], F32, name="scale_col")
         scaled_bias = keep.tile([P, FEAT], F32, name="scaled_bias")
         residual = [keep.tile([P, FEAT], F32, name="residual%d" % t) for t in range(ROW_TILES)]
 
-        def prepare_residuals():
+        def spread_scale():
             scale_bank = banks.tile([P, SPARE], F32, tag="bank", name="scale_bank")
-            nc.tensor.matmul(out=scale_bank[:], lhsT=ones[:], rhs=row0[:, FEAT:], start=True, stop=True)
-            nc.vector.tensor_copy(out=scale_col[:], in_=scale_bank[:, 0:1])
-            for h in range(HALVES):
-                cols = slice(h * BANK, (h + 1) * BANK)
-                bias_bank = banks.tile([P, BANK], F32, tag="bank", name="bias_bank")
-                nc.tensor.matmul(out=bias_bank[:], lhsT=ones[:], rhs=row0[:, cols], start=True, stop=True)
-                nc.vector.tensor_scalar(
-                    out=scaled_bias[:, cols], in0=bias_bank[:], scalar1=scale_col[:], scalar2=None, op0=ALU.mult
-                )
-            for t in range(ROW_TILES):
-                nc.gpsimd.tensor_tensor(out=residual[t][:], in0=x_tile(t), in1=scaled_bias[:], op=ALU.add)
+            nc.tensor.matmul(out=scale_bank[:], lhsT=ones[:, 0:P], rhs=row0[:, FEAT:], start=True, stop=True)
+            nc.scalar.copy(out=scale_col[:], in_=scale_bank[:, 0:1])
+
+        def spread_bias(h):
+            cols = slice(h * BANK, (h + 1) * BANK)
+            bias_bank = banks.tile([P, BANK], F32, tag="bank", name="bias_bank")
+            nc.tensor.matmul(out=bias_bank[:], lhsT=ones[:, 0:P], rhs=row0[:, cols], start=True, stop=True)
+            nc.scalar.activation(out=scaled_bias[:, cols], in_=bias_bank[:], func=ACT.Copy, scale=scale_col[:])
+
+        def warm(n):
+            warm_bank = banks.tile([P, BANK], F32, tag="bank", name="warm_bank")
+            for j in range(n):
+                nc.tensor.matmul(out=warm_bank[:], lhsT=ones[:, 0:P], rhs=ones[:], start=True, stop=True)
+
+        def prepare_residual(t):
+            nc.gpsimd.tensor_tensor(out=residual[t][:], in0=x_tile(t), in1=scaled_bias[:], op=ALU.add)
 
         def turn_bank(blocks, name):
             return banks.tile([P, blocks, P], F32, tag="bank", name=name)
@@ -123,9 +131,9 @@ def tile_reins_attention4_pa_kernel(tc, body, tokens, tfeat, Wf, b_f, scale, out
         def turn(dst, src):
             nc.tensor.transpose(out=dst, in_=src, identity=ident[:])
 
-        def group_words(grouped, bank, passes):
+        def group_words(grouped, bank):
             nc.scalar.copy(
-                out=grouped[:].bitcast(F32).rearrange("q (g r h) -> q g r h", g=passes, h=2),
+                out=grouped.bitcast(F32).rearrange("q g (r h) -> q g r h", h=2),
                 in_=bank[:].rearrange("q (g h) r -> q g r h", h=2),
             )
 
@@ -137,17 +145,24 @@ def tile_reins_attention4_pa_kernel(tc, body, tokens, tfeat, Wf, b_f, scale, out
             for dst, src in turns_into(x_bank, x_tile(t), FEAT_BLOCKS):
                 turn(dst, src)
             x_T[t] = ring.tile([P, FEAT_BLOCKS, P], F32, name="x_T", bufs=X_LEAD + 2)
-            if t % 2 == 0:
-                nc.vector.tensor_copy(out=x_T[t][:], in_=x_bank[:])
-            else:
-                nc.scalar.copy(out=x_T[t][:], in_=x_bank[:])
+            nc.vector.tensor_copy(out=x_T[t][:], in_=x_bank[:])
 
+        warm(WARM_MATMULS)
         turn_x_early(0)
         tok_banks = [banks.tile([P, TOKENS], F32, tag="bank", name="tok_bank%d" % b) for b in range(FEAT_BLOCKS)]
         for a in range(TOKENS // P):
             tok_words = tok_sb[:, a, :].bitcast(F32)
             for b in range(FEAT_BLOCKS):
                 turn(tok_banks[b][:, a * P : (a + 1) * P], tok_words[:, b * P : (b + 1) * P])
+            if a == 0:
+                warm(1)
+            elif a == 1:
+                spread_scale()
+                spread_bias(0)
+            elif a == 2:
+                spread_bias(1)
+        for t in range(ROW_TILES):
+            prepare_residual(t)
         for b in range(FEAT_BLOCKS):
             for e in range(2):
                 halves = tok_banks[b][:].bitcast(BF16).rearrange("q (m e) -> q e m", e=2)
@@ -155,7 +170,6 @@ def tile_reins_attention4_pa_kernel(tc, body, tokens, tfeat, Wf, b_f, scale, out
                     nc.vector.tensor_copy(out=tok_T[:, b, e, :], in_=halves[:, e, :])
                 else:
                     nc.scalar.copy(out=tok_T[:, b, e, :], in_=halves[:, e, :])
-        turn_x_early(1)
 
         row_max = keep.tile([P, ROW_TILES], F32, name="row_max")
         exp_bias = keep.tile([P, ROW_TILES], F32, name="exp_bias")
@@ -191,13 +205,15 @@ def tile_reins_attention4_pa_kernel(tc, body, tokens, tfeat, Wf, b_f, scale, out
         tf_codes = keep.tile([P, FEAT], U32, name="tf_codes", align_bytes=64)
         tf_scales = keep.tile([P, FEAT], U8, name="tf_scales", align_bytes=64)
 
-        def quantise_tfeat():
+        def group_tfeat():
             for h in range(HALVES):
                 cols = slice(h * BANK, (h + 1) * BANK)
                 nc.vector.tensor_copy(
                     out=tf_grouped[:, cols, :].rearrange("q (c i) j -> q c j i", i=4),
                     in_=tf_raw[:, :, cols].rearrange("q j (c i) -> q c j i", i=4),
                 )
+
+        def quantise_tfeat():
             for h in range(HALVES):
                 cols = slice(h * BANK, (h + 1) * BANK)
                 nc.vector.quantize_mx(
@@ -237,18 +253,17 @@ def tile_reins_attention4_pa_kernel(tc, body, tokens, tfeat, Wf, b_f, scale, out
 
         w_codes = keep.tile([P, FEAT_PASSES, FEAT], U32, name="w_codes", align_bytes=64)
         w_scales = keep.tile([P, FEAT_PASSES, FEAT], U8, name="w_scales", align_bytes=64)
-        w_grouped = {}
+        w_grouped = [
+            keep.tile([P, FEAT_PASSES, BANK * PACK], BF16, name="w_grouped%d" % h, align_bytes=64) for h in range(HALVES)
+        ]
         u_codes = [keep.tile([P, FEAT_PASSES, P], U32, name="u_codes%d" % t, align_bytes=64) for t in range(ROW_TILES)]
         u_scales = [keep.tile([P, FEAT_PASSES, P], U8, name="u_scales%d" % t, align_bytes=64) for t in range(ROW_TILES)]
 
-        def w_quantise(a):
-            rows = slice(a * P, (a + 1) * P)
-            for g in range(FEAT_PASSES):
-                nc.vector.quantize_mx(
-                    out=w_codes[:, g, rows].bitcast(FP8X4),
-                    scales=w_scales[:, g, rows],
-                    in_=w_grouped[a][:, g * P * PACK : (g + 1) * P * PACK],
-                )
+        def w_quantise(h, g):
+            rows = slice(h * BANK, (h + 1) * BANK)
+            nc.vector.quantize_mx(
+                out=w_codes[:, g, rows].bitcast(FP8X4), scales=w_scales[:, g, rows], in_=w_grouped[h][:, g, :]
+            )
 
         def project_passes(t, h):
             cols = slice(h * BANK, (h + 1) * BANK)
@@ -295,19 +310,20 @@ def tile_reins_attention4_pa_kernel(tc, body, tokens, tfeat, Wf, b_f, scale, out
             return 0 <= t < ROW_TILES
 
         for i in range(ROUNDS):
-            x_t, u_t, e_t = i + X_LEAD, i - U_LAG, i - E_LAG
-            w_now = [a for a in range(i * W_TILES_PER_ROUND, (i + 1) * W_TILES_PER_ROUND) if a < W_TILES]
-            for a in range((i - 1) * W_TILES_PER_ROUND, i * W_TILES_PER_ROUND):
-                if 0 <= a < W_TILES:
-                    w_quantise(a)
+            u_t, e_t = i - U_LAG, i - E_LAG
+            x_now = [t for t in ([1, 2] if i == 0 else [i + X_LEAD]) if t < ROW_TILES]
+            w_now = W_ROUNDS[i] if i < len(W_ROUNDS) else ()
+            if i in W_QUANTISE_ROUNDS:
+                for g in range(FEAT_PASSES):
+                    w_quantise(W_QUANTISE_ROUNDS.index(i), g)
 
             turns = []
+            x_banks = [turn_bank(FEAT_BLOCKS, "x_bank") for t in x_now]
+            for t, x_bank in zip(x_now, x_banks):
+                turns.extend(turns_into(x_bank, x_tile(t), FEAT_BLOCKS))
             w_banks = [turn_bank(FEAT_BLOCKS, "w_bank") for a in w_now]
             for a, w_bank in zip(w_now, w_banks):
                 turns.extend(turns_into(w_bank, w_tile(a), FEAT_BLOCKS))
-            if is_tile(x_t):
-                x_bank = turn_bank(FEAT_BLOCKS, "x_bank")
-                turns.extend(turns_into(x_bank, x_tile(x_t), FEAT_BLOCKS))
             if is_tile(u_t):
                 u_bank = turn_bank(FEAT_BLOCKS, "u_bank")
                 turns.extend(turns_into(u_bank, u_rows[u_t][:], FEAT_BLOCKS))
@@ -322,25 +338,25 @@ def tile_reins_attention4_pa_kernel(tc, body, tokens, tfeat, Wf, b_f, scale, out
                     score_pass(i, score_bank, k)
                     for place in range(max(k * RIDERS, first_place), (k + 1) * RIDERS):
                         turn(*turns[place - first_place])
+                if i == 1:
+                    group_tfeat()
                 nc.vector.tensor_reduce(out=row_max[:, i : i + 1], in_=score_bank[:], axis=AXIS.X, op=ALU.max)
             else:
                 for dst, src in turns:
                     turn(dst, src)
-            if i == 0:
-                prepare_residuals()
 
+            for t, x_bank in zip(x_now, x_banks):
+                x_T[t] = ring.tile([P, FEAT_BLOCKS, P], F32, name="x_T", bufs=X_LEAD + 2)
+                nc.scalar.copy(out=x_T[t][:], in_=x_bank[:])
             for a, w_bank in zip(w_now, w_banks):
-                w_grouped[a] = ring.tile([P, FEAT], BF16, name="w_grouped", bufs=2 * W_TILES_PER_ROUND, align_bytes=64)
-                group_words(w_grouped[a], w_bank, FEAT_PASSES)
-            if is_tile(x_t):
-                x_T[x_t] = ring.tile([P, FEAT_BLOCKS, P], F32, name="x_T", bufs=X_LEAD + 2)
-                nc.scalar.copy(out=x_T[x_t][:], in_=x_bank[:])
+                h, rows = a // W_TILES_PER_HALF, slice(a % W_TILES_PER_HALF * P * PACK, (a % W_TILES_PER_HALF + 1) * P * PACK)
+                group_words(w_grouped[h][:, :, rows], w_bank)
             if is_tile(u_t):
-                u_grouped = ring.tile([P, FEAT], BF16, name="u_grouped", align_bytes=64)
-                group_words(u_grouped, u_bank, FEAT_PASSES)
+                u_grouped = ring.tile([P, FEAT_PASSES, P * PACK], BF16, name="u_grouped", align_bytes=64)
+                group_words(u_grouped[:], u_bank)
             if is_tile(e_t):
-                e_grouped = ring.tile([P, P * PACK], BF16, name="e_grouped", align_bytes=64)
-                group_words(e_grouped, e_bank, 1)
+                e_grouped = ring.tile([P, 1, P * PACK], BF16, name="e_grouped", align_bytes=64)
+                group_words(e_grouped[:], e_bank)
             if is_tile(i):
                 softmax_numerators(i, score_bank)
 
@@ -350,13 +366,13 @@ def tile_reins_attention4_pa_kernel(tc, body, tokens, tfeat, Wf, b_f, scale, out
                 nc.vector.quantize_mx(
                     out=u_codes[u_t][:].rearrange("q g r -> q (g r)").bitcast(FP8X4),
                     scales=u_scales[u_t][:].rearrange("q g r -> q (g r)"),
-                    in_=u_grouped[:],
+                    in_=u_grouped[:].rearrange("q g c -> q (g c)"),
                 )
             if is_tile(e_t):
                 e_codes[e_t] = ring.tile([P, P], U32, name="e_codes", align_bytes=64)
                 e_scales[e_t] = ring.tile([P, P], U8, name="e_scales", align_bytes=64)
                 nc.vector.quantize_mx(
-                    out=e_codes[e_t][:].bitcast(FP8X4), scales=e_scales[e_t][:], in_=e_grouped[:]
+                    out=e_codes[e_t][:].bitcast(FP8X4), scales=e_scales[e_t][:], in_=e_grouped[:, 0, :]
                 )
 
             if is_tile(i - ATTEND_LAG):

@@ -34,8 +34,8 @@ PROJECT_LAG = 6
 ROUNDS = ROW_TILES + PROJECT_LAG
 W_TILES = FEAT // P
 W_TILES_PER_HALF = W_TILES // HALVES
-W_ROUNDS = ((0,), (1, 2), (3, 4), (5, 6), (7,))
-W_QUANTISE_ROUNDS = (3, 5)
+W_ROUNDS = ((0,), (1,), (2, 3), (4, 5), (6,), (7,))
+W_QUANTISE_ROUNDS = (3, 6)
 WARM_MATMULS = 4
 RIDERS = 2
 
@@ -90,28 +90,33 @@ def tile_reins_attention4_pa_kernel(tc, body, tokens, tfeat, Wf, b_f, scale, out
 
         ident = keep.tile([P, P], F32, name="ident")
         make_identity(nc, ident[:])
-        ones = keep.tile([P, BANK], BF16, name="ones")
-        nc.vector.memset(ones[:], 1.0)
 
         SPARE = 32
         row0 = keep.tile([P, FEAT + SPARE], BF16, name="row0")
         nc.vector.memset(row0[:].bitcast(U32), 0)
+        ones = keep.tile([P, BANK], BF16, name="ones")
+        nc.vector.memset(ones[:], 1.0)
         nc.scalar.dma_start(out=row0[0:1, 0:FEAT], in_=b_f.unsqueeze(0))
         nc.scalar.dma_start(out=row0[0:1, FEAT : FEAT + 1], in_=scale.unsqueeze(0))
         scale_col = keep.tile([P, 1], F32, name="scale_col")
         scaled_bias = keep.tile([P, FEAT], F32, name="scaled_bias")
         residual = [keep.tile([P, FEAT], F32, name="residual%d" % t) for t in range(ROW_TILES)]
 
-        def spread_scale():
+        def spread_rows():
             scale_bank = banks.tile([P, SPARE], F32, tag="bank", name="scale_bank")
             nc.tensor.matmul(out=scale_bank[:], lhsT=ones[:, 0:P], rhs=row0[:, FEAT:], start=True, stop=True)
             nc.scalar.copy(out=scale_col[:], in_=scale_bank[:, 0:1])
+            bias_banks = []
+            for h in range(HALVES):
+                bias_bank = banks.tile([P, BANK], F32, tag="bank", name="bias_bank%d" % h)
+                bias_row = row0[:, h * BANK : (h + 1) * BANK]
+                nc.tensor.matmul(out=bias_bank[:], lhsT=ones[:, 0:P], rhs=bias_row, start=True, stop=True)
+                bias_banks.append(bias_bank)
+            return bias_banks
 
-        def spread_bias(h):
+        def scale_bias(h):
             cols = slice(h * BANK, (h + 1) * BANK)
-            bias_bank = banks.tile([P, BANK], F32, tag="bank", name="bias_bank")
-            nc.tensor.matmul(out=bias_bank[:], lhsT=ones[:, 0:P], rhs=row0[:, cols], start=True, stop=True)
-            nc.scalar.activation(out=scaled_bias[:, cols], in_=bias_bank[:], func=ACT.Copy, scale=scale_col[:])
+            nc.scalar.activation(out=scaled_bias[:, cols], in_=bias_banks[h][:], func=ACT.Copy, scale=scale_col[:])
 
         def warm(n):
             warm_bank = banks.tile([P, BANK], F32, tag="bank", name="warm_bank")
@@ -137,7 +142,7 @@ def tile_reins_attention4_pa_kernel(tc, body, tokens, tfeat, Wf, b_f, scale, out
                 in_=bank[:].rearrange("q (g h) r -> q g r h", h=2),
             )
 
-        tok_T = keep.tile([P, FEAT_BLOCKS, 2, TOKENS], BF16, name="tok_T")
+        tok_T = keep.tile([P, TOKENS // P, FEAT_BLOCKS, 2, P], BF16, name="tok_T")
         x_T = {}
 
         def turn_x_early(t):
@@ -147,46 +152,26 @@ def tile_reins_attention4_pa_kernel(tc, body, tokens, tfeat, Wf, b_f, scale, out
             x_T[t] = ring.tile([P, FEAT_BLOCKS, P], F32, name="x_T", bufs=X_LEAD + 2)
             nc.vector.tensor_copy(out=x_T[t][:], in_=x_bank[:])
 
-        warm(WARM_MATMULS)
-        turn_x_early(0)
-        tok_banks = [banks.tile([P, TOKENS], F32, tag="bank", name="tok_bank%d" % b) for b in range(FEAT_BLOCKS)]
-        for a in range(TOKENS // P):
-            tok_words = tok_sb[:, a, :].bitcast(F32)
-            for b in range(FEAT_BLOCKS):
-                turn(tok_banks[b][:, a * P : (a + 1) * P], tok_words[:, b * P : (b + 1) * P])
-            if a == 0:
-                warm(1)
-            elif a == 1:
-                spread_scale()
-                spread_bias(0)
-            elif a == 2:
-                spread_bias(1)
-        for t in range(ROW_TILES):
-            prepare_residual(t)
-        for b in range(FEAT_BLOCKS):
-            for e in range(2):
-                halves = tok_banks[b][:].bitcast(BF16).rearrange("q (m e) -> q e m", e=2)
-                if b % 2 == 0:
-                    nc.vector.tensor_copy(out=tok_T[:, b, e, :], in_=halves[:, e, :])
-                else:
-                    nc.scalar.copy(out=tok_T[:, b, e, :], in_=halves[:, e, :])
-
         row_max = keep.tile([P, ROW_TILES], F32, name="row_max")
         exp_bias = keep.tile([P, ROW_TILES], F32, name="exp_bias")
         e_sum = keep.tile([P, ROW_TILES], F32, name="e_sum")
         e_sum_inv = keep.tile([P, ROW_TILES], F32, name="e_sum_inv")
         e_rows = {}
 
-        def score_pass(t, bank, k):
-            block, e = 2 * (k // 4) + k % 2, k % 4 // 2
+        def score_pass(t, bank, k, tiles):
+            block, e = k // 2, k % 2
             x_halves = x_T[t][:].bitcast(BF16).rearrange("q b (r e) -> q b r e", e=2)
             nc.tensor.matmul(
-                out=bank[:],
+                out=bank[:, tiles, :],
                 lhsT=x_halves[:, block, :, e],
-                rhs=tok_T[:, block, e, :],
+                rhs=tok_T[:, tiles, block, e, :],
                 start=(k == 0),
                 stop=(k == SCORE_PASSES - 1),
             )
+
+        def score_tokens(a):
+            for k in range(SCORE_PASSES):
+                score_pass(0, score_bank, k, slice(a, a + 1))
 
         def softmax_numerators(t, bank):
             col = slice(t, t + 1)
@@ -194,12 +179,44 @@ def tile_reins_attention4_pa_kernel(tc, body, tokens, tfeat, Wf, b_f, scale, out
             e_rows[t] = ring.tile([P, TOKENS], BF16, name="e_rows")
             nc.scalar.activation(
                 out=e_rows[t][:],
-                in_=bank[:],
+                in_=bank[:].rearrange("p a m -> p (a m)"),
                 func=ACT.Exp,
                 bias=exp_bias[:, col],
                 scale=SCORE_SCALE,
                 accum_out=e_sum[:, col],
             )
+
+        warm(WARM_MATMULS)
+        turn_x_early(0)
+        bias_banks = spread_rows()
+        def turn_tokens(a):
+            tok_words = tok_sb[:, a, :].bitcast(F32)
+            for half in range(2):
+                blocks = slice(2 * half, 2 * half + 2)
+                tok_bank = banks.tile([P, 2, P], F32, tag="bank", name="tok_bank")
+                for j in range(2):
+                    b = 2 * half + j
+                    turn(tok_bank[:, j, :], tok_words[:, b * P : (b + 1) * P])
+                halves = tok_bank[:].rearrange("q b m -> q (b m)").bitcast(BF16)
+                halves = halves.rearrange("q (b m e) -> q b e m", b=2, e=2)
+                if half == 0:
+                    nc.vector.tensor_copy(out=tok_T[:, a, blocks, :, :], in_=halves)
+                else:
+                    nc.scalar.copy(out=tok_T[:, a, blocks, :, :], in_=halves)
+
+        score_bank = banks.tile([P, TOKENS // P, P], F32, tag="bank", name="score_bank")
+        for a in range(3):
+            turn_tokens(a)
+        score_tokens(0)
+        turn_tokens(3)
+        score_tokens(1)
+        for h in range(HALVES):
+            scale_bias(h)
+        for t in range(ROW_TILES):
+            prepare_residual(t)
+        turn_x_early(1)
+        score_tokens(2)
+        score_tokens(3)
 
         tf_grouped = keep.tile([P, FEAT, PACK], BF16, name="tf_grouped", align_bytes=64)
         tf_codes = keep.tile([P, FEAT], U32, name="tf_codes", align_bytes=64)
@@ -311,7 +328,7 @@ def tile_reins_attention4_pa_kernel(tc, body, tokens, tfeat, Wf, b_f, scale, out
 
         for i in range(ROUNDS):
             u_t, e_t = i - U_LAG, i - E_LAG
-            x_now = [t for t in ([1, 2] if i == 0 else [i + X_LEAD]) if t < ROW_TILES]
+            x_now = [t for t in [i + X_LEAD] if t < ROW_TILES]
             w_now = W_ROUNDS[i] if i < len(W_ROUNDS) else ()
             if i in W_QUANTISE_ROUNDS:
                 for g in range(FEAT_PASSES):
@@ -331,16 +348,18 @@ def tile_reins_attention4_pa_kernel(tc, body, tokens, tfeat, Wf, b_f, scale, out
                 e_bank = turn_bank(TOKENS // 2 // P, "e_bank")
                 turns.extend(turns_into(e_bank, e_rows[e_t][:], TOKENS // 2 // P))
             if is_tile(i):
-                first_place = RIDERS * SCORE_PASSES - len(turns)
+                if i > 0:
+                    score_bank = banks.tile([P, TOKENS // P, P], F32, tag="bank", name="score_bank")
+                first_place = RIDERS * (SCORE_PASSES - 1) - len(turns)
                 assert first_place >= 0
-                score_bank = banks.tile([P, TOKENS], F32, tag="bank", name="score_bank")
                 for k in range(SCORE_PASSES):
-                    score_pass(i, score_bank, k)
-                    for place in range(max(k * RIDERS, first_place), (k + 1) * RIDERS):
+                    if i > 0:
+                        score_pass(i, score_bank, k, slice(0, TOKENS // P))
+                    for place in range(max(k * RIDERS, first_place), min(k + 1, SCORE_PASSES - 1) * RIDERS):
                         turn(*turns[place - first_place])
                 if i == 1:
                     group_tfeat()
-                nc.vector.tensor_reduce(out=row_max[:, i : i + 1], in_=score_bank[:], axis=AXIS.X, op=ALU.max)
+                nc.vector.tensor_reduce(out=row_max[:, i : i + 1], in_=score_bank[:].rearrange("p a m -> p (a m)"), axis=AXIS.X, op=ALU.max)
             else:
                 for dst, src in turns:
                     turn(dst, src)

@@ -36,6 +36,7 @@ W_TILES = FEAT // P
 W_TILES_PER_HALF = W_TILES // HALVES
 W_ROUNDS = ((0,), (1,), (2, 3), (4, 5), (6,), (7,))
 W_QUANTISE_ROUNDS = (3, 6)
+LAST_WIDTH = 256
 WARM_MATMULS = 4
 RIDERS = 2
 
@@ -142,7 +143,7 @@ def tile_reins_attention4_pa_kernel(tc, body, tokens, tfeat, Wf, b_f, scale, out
                 in_=bank[:].rearrange("q (g h) r -> q g r h", h=2),
             )
 
-        tok_T = keep.tile([P, TOKENS // P, FEAT_BLOCKS, 2, P], BF16, name="tok_T")
+        tok_T = keep.tile([P, 2, FEAT_BLOCKS, 2, 2 * P], BF16, name="tok_T")
         x_T = {}
 
         def turn_x_early(t):
@@ -152,45 +153,46 @@ def tile_reins_attention4_pa_kernel(tc, body, tokens, tfeat, Wf, b_f, scale, out
             x_T[t] = ring.tile([P, FEAT_BLOCKS, P], F32, name="x_T", bufs=X_LEAD + 2)
             nc.vector.tensor_copy(out=x_T[t][:], in_=x_bank[:])
 
-        row_max = keep.tile([P, ROW_TILES], F32, name="row_max")
-        exp_bias = keep.tile([P, ROW_TILES], F32, name="exp_bias")
+        neg_max = keep.tile([P, ROW_TILES], F32, name="neg_max")
         e_sum = keep.tile([P, ROW_TILES], F32, name="e_sum")
         e_sum_inv = keep.tile([P, ROW_TILES], F32, name="e_sum_inv")
         e_rows = {}
 
-        def score_pass(t, bank, k, tiles):
+        def score_pass(t, bank, k, halves):
             block, e = k // 2, k % 2
             x_halves = x_T[t][:].bitcast(BF16).rearrange("q b (r e) -> q b r e", e=2)
             nc.tensor.matmul(
-                out=bank[:, tiles, :],
+                out=bank[:, halves, :],
                 lhsT=x_halves[:, block, :, e],
-                rhs=tok_T[:, tiles, block, e, :],
+                rhs=tok_T[:, halves, block, e, :],
                 start=(k == 0),
                 stop=(k == SCORE_PASSES - 1),
             )
 
-        def score_tokens(a):
+        def score_half(h):
             for k in range(SCORE_PASSES):
-                score_pass(0, score_bank, k, slice(a, a + 1))
+                score_pass(0, score_bank, k, slice(h, h + 1))
+
+        def invert_sum(t):
+            col = slice(t, t + 1)
+            nc.vector.reciprocal(out=e_sum_inv[:, col], in_=e_sum[:, col])
 
         def softmax_numerators(t, bank):
             col = slice(t, t + 1)
-            nc.scalar.mul(out=exp_bias[:, col], in_=row_max[:, col], mul=-SCORE_SCALE)
             e_rows[t] = ring.tile([P, TOKENS], BF16, name="e_rows")
             nc.scalar.activation(
                 out=e_rows[t][:],
                 in_=bank[:].rearrange("p a m -> p (a m)"),
                 func=ACT.Exp,
-                bias=exp_bias[:, col],
-                scale=SCORE_SCALE,
+                bias=neg_max[:, col],
                 accum_out=e_sum[:, col],
             )
 
         warm(WARM_MATMULS)
         turn_x_early(0)
-        bias_banks = spread_rows()
         def turn_tokens(a):
             tok_words = tok_sb[:, a, :].bitcast(F32)
+            cols = slice(a % 2 * P, (a % 2 + 1) * P)
             for half in range(2):
                 blocks = slice(2 * half, 2 * half + 2)
                 tok_bank = banks.tile([P, 2, P], F32, tag="bank", name="tok_bank")
@@ -200,23 +202,25 @@ def tile_reins_attention4_pa_kernel(tc, body, tokens, tfeat, Wf, b_f, scale, out
                 halves = tok_bank[:].rearrange("q b m -> q (b m)").bitcast(BF16)
                 halves = halves.rearrange("q (b m e) -> q b e m", b=2, e=2)
                 if half == 0:
-                    nc.vector.tensor_copy(out=tok_T[:, a, blocks, :, :], in_=halves)
+                    nc.vector.tensor_scalar(
+                        out=tok_T[:, a // 2, blocks, :, cols], in0=halves, scalar1=SCORE_SCALE, scalar2=None, op0=ALU.mult
+                    )
                 else:
-                    nc.scalar.copy(out=tok_T[:, a, blocks, :, :], in_=halves)
+                    nc.scalar.activation(
+                        out=tok_T[:, a // 2, blocks, :, cols], in_=halves, func=ACT.Copy, scale=SCORE_SCALE
+                    )
 
-        score_bank = banks.tile([P, TOKENS // P, P], F32, tag="bank", name="score_bank")
-        for a in range(3):
+        score_bank = banks.tile([P, 2, 2 * P], F32, tag="bank", name="score_bank")
+        for a in range(TOKENS // P):
             turn_tokens(a)
-        score_tokens(0)
-        turn_tokens(3)
-        score_tokens(1)
+        bias_banks = spread_rows()
+        turn_x_early(1)
+        for h in range(2):
+            score_half(h)
         for h in range(HALVES):
             scale_bias(h)
         for t in range(ROW_TILES):
             prepare_residual(t)
-        turn_x_early(1)
-        score_tokens(2)
-        score_tokens(3)
 
         tf_grouped = keep.tile([P, FEAT, PACK], BF16, name="tf_grouped", align_bytes=64)
         tf_codes = keep.tile([P, FEAT], U32, name="tf_codes", align_bytes=64)
@@ -245,7 +249,6 @@ def tile_reins_attention4_pa_kernel(tc, body, tokens, tfeat, Wf, b_f, scale, out
 
         def attend(t):
             col = slice(t, t + 1)
-            nc.vector.reciprocal(out=e_sum_inv[:, col], in_=e_sum[:, col])
             u_rows[t] = ring.tile([P, FEAT], BF16, name="u_rows", bufs=U_LAG - ATTEND_LAG + 2)
             for h in range(HALVES):
                 cols = slice(h * BANK, (h + 1) * BANK)
@@ -282,9 +285,9 @@ def tile_reins_attention4_pa_kernel(tc, body, tokens, tfeat, Wf, b_f, scale, out
                 out=w_codes[:, g, rows].bitcast(FP8X4), scales=w_scales[:, g, rows], in_=w_grouped[h][:, g, :]
             )
 
-        def project_passes(t, h):
-            cols = slice(h * BANK, (h + 1) * BANK)
-            bank = banks.tile([P, BANK], F32, tag="bank", name="y_bank")
+        def project_passes(t, first, width):
+            cols = slice(first, first + width)
+            bank = banks.tile([P, width], F32, tag="bank", name="y_bank")
             for g in range(FEAT_PASSES):
                 nc.tensor.matmul_mx(
                     out=bank[:],
@@ -297,36 +300,73 @@ def tile_reins_attention4_pa_kernel(tc, body, tokens, tfeat, Wf, b_f, scale, out
                 )
             return bank
 
-        def finish_on_vector(t, h, bank):
-            cols = slice(h * BANK, (h + 1) * BANK)
-            result = ring.tile([P, BANK], F32, name="result", bufs=4)
+        def finish_on_vector(t, first, width, bank, queue):
+            cols = slice(first, first + width)
+            result = ring.tile([P, BANK], F32, name="result", bufs=8)
             nc.vector.scalar_tensor_tensor(
-                out=result[:], in0=bank[:], scalar=scale_col[:], in1=residual[t][:, cols], op0=ALU.mult, op1=ALU.add
+                out=result[:, 0:width],
+                in0=bank[:],
+                scalar=scale_col[:],
+                in1=residual[t][:, cols],
+                op0=ALU.mult,
+                op1=ALU.add,
             )
-            nc.sync.dma_start(out=out_rows[:, t, cols], in_=result[:])
+            queue.dma_start(out=out_rows[:, t, cols], in_=result[:, 0:width])
 
-        def finish_beside_vector(t, h, bank):
-            cols = slice(h * BANK, (h + 1) * BANK)
-            scaled = ring.tile([P, BANK], F32, name="scaled")
+        def finish_beside_vector(t, first, width, bank):
+            cols = slice(first, first + width)
+            scaled = ring.tile([P, width], F32, name="scaled")
             nc.scalar.activation(out=scaled[:], in_=bank[:], func=ACT.Copy, scale=scale_col[:])
-            result = ring.tile([P, BANK], F32, name="result_beside")
+            result = ring.tile([P, width], F32, name="result_beside", bufs=6)
             nc.gpsimd.tensor_tensor(out=result[:], in0=scaled[:], in1=residual[t][:, cols], op=ALU.add)
             nc.sync.dma_start(out=out_rows[:, t, cols], in_=result[:])
 
+        def project_banks(t):
+            return [project_passes(t, h * BANK, BANK) for h in range(HALVES)]
+
+        def finish(t, y_banks):
+            finish_on_vector(t, BANK, BANK, y_banks[1], nc.sync)
+            finish_beside_vector(t, 0, BANK, y_banks[0])
+
         def project(t):
-            first_bank = project_passes(t, 0)
-            second_bank = project_passes(t, 1)
-            if t == ROW_TILES - 1:
-                finish_on_vector(t, 0, first_bank)
-                finish_on_vector(t, 1, second_bank)
-            else:
-                finish_on_vector(t, 1, second_bank)
-                finish_beside_vector(t, 0, first_bank)
+            finish(t, project_banks(t))
+
+        def project_beside_none(t):
+            y_banks = project_banks(t)
+            for h in range(HALVES):
+                finish_on_vector(t, h * BANK, BANK, y_banks[h], nc.sync)
+
+        def project_last(t):
+            for first in range(0, FEAT, LAST_WIDTH):
+                finish_on_vector(t, first, LAST_WIDTH, project_passes(t, first, LAST_WIDTH), nc.scalar)
 
         def is_tile(t):
             return 0 <= t < ROW_TILES
 
-        for i in range(ROUNDS):
+        def empty_u_bank(t, bank):
+            u_grouped[t] = ring.tile([P, FEAT_PASSES, P * PACK], BF16, name="u_grouped", align_bytes=256)
+            group_words(u_grouped[t][:], bank)
+
+        def empty_e_bank(t, bank):
+            e_grouped[t] = ring.tile([P, 1, P * PACK], BF16, name="e_grouped", align_bytes=256)
+            group_words(e_grouped[t][:], bank)
+
+        u_grouped = {}
+        e_grouped = {}
+
+        def quantise_u(t):
+            nc.vector.quantize_mx(
+                out=u_codes[t][:].rearrange("q g r -> q (g r)").bitcast(FP8X4),
+                scales=u_scales[t][:].rearrange("q g r -> q (g r)"),
+                in_=u_grouped[t][:].rearrange("q g c -> q (g c)"),
+            )
+
+        def quantise_e(t):
+            e_codes[t] = ring.tile([P, P], U32, name="e_codes", align_bytes=256)
+            e_scales[t] = ring.tile([P, P], U8, name="e_scales", align_bytes=256)
+            nc.vector.quantize_mx(out=e_codes[t][:].bitcast(FP8X4), scales=e_scales[t][:], in_=e_grouped[t][:, 0, :])
+
+        for i in range(ROW_TILES):
             u_t, e_t = i - U_LAG, i - E_LAG
             x_now = [t for t in [i + X_LEAD] if t < ROW_TILES]
             w_now = W_ROUNDS[i] if i < len(W_ROUNDS) else ()
@@ -349,17 +389,25 @@ def tile_reins_attention4_pa_kernel(tc, body, tokens, tfeat, Wf, b_f, scale, out
                 turns.extend(turns_into(e_bank, e_rows[e_t][:], TOKENS // 2 // P))
             if is_tile(i):
                 if i > 0:
-                    score_bank = banks.tile([P, TOKENS // P, P], F32, tag="bank", name="score_bank")
+                    score_bank = banks.tile([P, 2, 2 * P], F32, tag="bank", name="score_bank")
                 first_place = RIDERS * (SCORE_PASSES - 1) - len(turns)
                 assert first_place >= 0
                 for k in range(SCORE_PASSES):
                     if i > 0:
-                        score_pass(i, score_bank, k, slice(0, TOKENS // P))
+                        score_pass(i, score_bank, k, slice(0, 2))
                     for place in range(max(k * RIDERS, first_place), min(k + 1, SCORE_PASSES - 1) * RIDERS):
                         turn(*turns[place - first_place])
                 if i == 1:
                     group_tfeat()
-                nc.vector.tensor_reduce(out=row_max[:, i : i + 1], in_=score_bank[:].rearrange("p a m -> p (a m)"), axis=AXIS.X, op=ALU.max)
+                if i > 0:
+                    invert_sum(i - 1)
+                nc.vector.tensor_reduce(
+                    out=neg_max[:, i : i + 1],
+                    in_=score_bank[:].rearrange("p a m -> p (a m)"),
+                    axis=AXIS.X,
+                    op=ALU.max,
+                    negate=True,
+                )
             else:
                 for dst, src in turns:
                     turn(dst, src)
@@ -371,30 +419,52 @@ def tile_reins_attention4_pa_kernel(tc, body, tokens, tfeat, Wf, b_f, scale, out
                 h, rows = a // W_TILES_PER_HALF, slice(a % W_TILES_PER_HALF * P * PACK, (a % W_TILES_PER_HALF + 1) * P * PACK)
                 group_words(w_grouped[h][:, :, rows], w_bank)
             if is_tile(u_t):
-                u_grouped = ring.tile([P, FEAT_PASSES, P * PACK], BF16, name="u_grouped", align_bytes=64)
-                group_words(u_grouped[:], u_bank)
+                empty_u_bank(u_t, u_bank)
             if is_tile(e_t):
-                e_grouped = ring.tile([P, 1, P * PACK], BF16, name="e_grouped", align_bytes=64)
-                group_words(e_grouped[:], e_bank)
+                empty_e_bank(e_t, e_bank)
             if is_tile(i):
                 softmax_numerators(i, score_bank)
 
             if i == 1:
                 quantise_tfeat()
             if is_tile(u_t):
-                nc.vector.quantize_mx(
-                    out=u_codes[u_t][:].rearrange("q g r -> q (g r)").bitcast(FP8X4),
-                    scales=u_scales[u_t][:].rearrange("q g r -> q (g r)"),
-                    in_=u_grouped[:].rearrange("q g c -> q (g c)"),
-                )
+                quantise_u(u_t)
             if is_tile(e_t):
-                e_codes[e_t] = ring.tile([P, P], U32, name="e_codes", align_bytes=64)
-                e_scales[e_t] = ring.tile([P, P], U8, name="e_scales", align_bytes=64)
-                nc.vector.quantize_mx(
-                    out=e_codes[e_t][:].bitcast(FP8X4), scales=e_scales[e_t][:], in_=e_grouped[:, 0, :]
-                )
+                quantise_e(e_t)
 
             if is_tile(i - ATTEND_LAG):
                 attend(i - ATTEND_LAG)
             if is_tile(i - PROJECT_LAG):
                 project(i - PROJECT_LAG)
+
+        def turn_u(t):
+            bank = turn_bank(FEAT_BLOCKS, "u_bank")
+            for dst, src in turns_into(bank, u_rows[t][:], FEAT_BLOCKS):
+                turn(dst, src)
+            empty_u_bank(t, bank)
+
+        def turn_e(t):
+            bank = turn_bank(TOKENS // 2 // P, "e_bank")
+            for dst, src in turns_into(bank, e_rows[t][:], TOKENS // 2 // P):
+                turn(dst, src)
+            empty_e_bank(t, bank)
+
+        invert_sum(7)
+        attend(6)
+        project(2)
+        turn_e(7)
+        turn_u(4)
+        turn_u(5)
+        turn_u(6)
+        quantise_e(7)
+        quantise_u(4)
+        quantise_u(5)
+        project(3)
+        attend(7)
+        quantise_u(6)
+        project(4)
+        project(5)
+        turn_u(7)
+        quantise_u(7)
+        project_beside_none(6)
+        project_last(7)

@@ -125,7 +125,11 @@ def tile_reins_attention4_pa_kernel(tc, body, tokens, tfeat, Wf, b_f, scale, out
                 nc.tensor.matmul(out=warm_bank[:], lhsT=ones[:, 0:P], rhs=ones[:], start=True, stop=True)
 
         def prepare_residual(t):
-            nc.gpsimd.tensor_tensor(out=residual[t][:], in0=x_tile(t), in1=scaled_bias[:], op=ALU.add)
+            for h in range(HALVES):
+                cols = slice(h * BANK, (h + 1) * BANK)
+                nc.gpsimd.tensor_tensor(
+                    out=residual[t][:, cols], in0=x_tile(t)[:, cols], in1=scaled_bias[:, cols], op=ALU.add
+                )
 
         def turn_bank(blocks, name):
             return banks.tile([P, blocks, P], F32, tag="bank", name=name)

@@ -35,7 +35,7 @@ ROUNDS = ROW_TILES + PROJECT_LAG
 W_TILES = FEAT // P
 W_TILES_PER_HALF = W_TILES // HALVES
 W_ROUNDS = ((0,), (1,), (2, 3), (4, 5), (6,), (7,))
-W_QUANTISE_ROUNDS = (3, 6)
+W_QUANTISE_ROUNDS = (3, 4, 6)
 LAST_WIDTH = 256
 WARM_MATMULS = 4
 RIDERS = 2
@@ -375,8 +375,9 @@ def tile_reins_attention4_pa_kernel(tc, body, tokens, tfeat, Wf, b_f, scale, out
             x_now = [t for t in [i + X_LEAD] if t < ROW_TILES]
             w_now = W_ROUNDS[i] if i < len(W_ROUNDS) else ()
             if i in W_QUANTISE_ROUNDS:
-                for g in range(FEAT_PASSES):
-                    w_quantise(W_QUANTISE_ROUNDS.index(i), g)
+                w_quantise(*divmod(W_QUANTISE_ROUNDS.index(i), FEAT_PASSES))
+                if i == W_QUANTISE_ROUNDS[-1]:
+                    w_quantise(1, 1)
 
             turns = []
             x_banks = [turn_bank(FEAT_BLOCKS, "x_bank") for t in x_now]
@@ -467,7 +468,7 @@ def tile_reins_attention4_pa_kernel(tc, body, tokens, tfeat, Wf, b_f, scale, out
         attend(7)
         quantise_u(6)
         project(4)
-        project(5)
+        project_beside_none(5)
         turn_u(7)
         quantise_u(7)
         project_beside_none(6)

@@ -26,7 +26,7 @@ HALVES = FEAT // BANK
 SCORE_SCALE = FEAT ** -0.5
 SCORE_PASSES = FEAT // P
 
-X_LEAD = 2
+X_LEAD = 1
 E_LAG = 1
 ATTEND_LAG = 2
 U_LAG = 4
@@ -34,10 +34,11 @@ PROJECT_LAG = 6
 ROUNDS = ROW_TILES + PROJECT_LAG
 W_TILES = FEAT // P
 W_TILES_PER_HALF = W_TILES // HALVES
-W_ROUNDS = ((0,), (1,), (2, 3), (4, 5), (6,), (7,))
+W_ROUNDS = ((), (0, 1), (2, 3), (4, 5), (6,), (7,))
 W_QUANTISE_ROUNDS = (3, 4, 6)
 LAST_WIDTH = 256
 WARM_MATMULS = 4
+TF_PIECE = 256
 RIDERS = 2
 
 FLOPS = 2 * ROWS * FEAT * TOKENS + 2 * ROWS * TOKENS * FEAT + 2 * ROWS * FEAT * FEAT
@@ -71,14 +72,14 @@ def tile_reins_attention4_pa_kernel(tc, body, tokens, tfeat, Wf, b_f, scale, out
         for a in range(TOKENS // P):
             nc.sync.dma_start(out=tok_sb[:, a, :], in_=tok_rows[:, a, :])
         nc.sync.dma_start(out=x_pairs[0][:, 1, :], in_=x_rows[:, 1, :])
-        load_x(1)
-        load_w(0)
         nc.sync.dma_start(
             out=tf_raw[:].rearrange("q (h e) c -> q h (e c)", e=2),
             in_=tfeat.rearrange("(h q e) c -> q h (e c)", h=2, e=2),
         )
-        load_x(2)
+        load_x(1)
+        load_w(0)
         load_w(1)
+        load_x(2)
         load_w(2)
         load_x(3)
         load_w(3)
@@ -218,9 +219,9 @@ def tile_reins_attention4_pa_kernel(tc, body, tokens, tfeat, Wf, b_f, scale, out
         for a in range(TOKENS // P):
             turn_tokens(a)
         bias_banks = spread_rows()
+        score_half(0)
         turn_x_early(1)
-        for h in range(2):
-            score_half(h)
+        score_half(1)
         for h in range(HALVES):
             scale_bias(h)
         for t in range(ROW_TILES):
@@ -230,22 +231,20 @@ def tile_reins_attention4_pa_kernel(tc, body, tokens, tfeat, Wf, b_f, scale, out
         tf_codes = keep.tile([P, FEAT], U32, name="tf_codes", align_bytes=64)
         tf_scales = keep.tile([P, FEAT], U8, name="tf_scales", align_bytes=64)
 
-        def group_tfeat():
-            for h in range(HALVES):
-                cols = slice(h * BANK, (h + 1) * BANK)
-                nc.vector.tensor_copy(
-                    out=tf_grouped[:, cols, :].rearrange("q (c i) j -> q c j i", i=4),
-                    in_=tf_raw[:, :, cols].rearrange("q j (c i) -> q c j i", i=4),
-                )
+        def group_tfeat(copy, piece):
+            cols = slice(piece * TF_PIECE, (piece + 1) * TF_PIECE)
+            copy(
+                out=tf_grouped[:, cols, :].rearrange("q (c i) j -> q c j i", i=4),
+                in_=tf_raw[:, :, cols].rearrange("q j (c i) -> q c j i", i=4),
+            )
 
-        def quantise_tfeat():
-            for h in range(HALVES):
-                cols = slice(h * BANK, (h + 1) * BANK)
-                nc.vector.quantize_mx(
-                    out=tf_codes[:, cols].bitcast(FP8X4),
-                    scales=tf_scales[:, cols],
-                    in_=tf_grouped[:, cols, :].rearrange("q c j -> q (c j)"),
-                )
+        def quantise_tfeat(h):
+            cols = slice(h * BANK, (h + 1) * BANK)
+            nc.vector.quantize_mx(
+                out=tf_codes[:, cols].bitcast(FP8X4),
+                scales=tf_scales[:, cols],
+                in_=tf_grouped[:, cols, :].rearrange("q c j -> q (c j)"),
+            )
 
         e_codes = {}
         e_scales = {}
@@ -372,7 +371,7 @@ def tile_reins_attention4_pa_kernel(tc, body, tokens, tfeat, Wf, b_f, scale, out
 
         for i in range(ROW_TILES):
             u_t, e_t = i - U_LAG, i - E_LAG
-            x_now = [t for t in [i + X_LEAD] if t < ROW_TILES]
+            x_now = [t for t in [i + X_LEAD] if 2 <= t < ROW_TILES]
             w_now = W_ROUNDS[i] if i < len(W_ROUNDS) else ()
             if i in W_QUANTISE_ROUNDS:
                 w_quantise(*divmod(W_QUANTISE_ROUNDS.index(i), FEAT_PASSES))
@@ -402,8 +401,6 @@ def tile_reins_attention4_pa_kernel(tc, body, tokens, tfeat, Wf, b_f, scale, out
                         score_pass(i, score_bank, k, slice(0, 2))
                     for place in range(max(k * RIDERS, first_place), min(k + 1, SCORE_PASSES - 1) * RIDERS):
                         turn(*turns[place - first_place])
-                if i == 1:
-                    group_tfeat()
                 if i > 0:
                     invert_sum(i - 1)
                 nc.vector.tensor_reduce(
@@ -430,8 +427,14 @@ def tile_reins_attention4_pa_kernel(tc, body, tokens, tfeat, Wf, b_f, scale, out
             if is_tile(i):
                 softmax_numerators(i, score_bank)
 
+            if i == 0:
+                group_tfeat(nc.vector.tensor_copy, 0)
+                group_tfeat(nc.vector.tensor_copy, 2)
+                group_tfeat(nc.vector.tensor_copy, 3)
+                group_tfeat(nc.scalar.copy, 1)
+                quantise_tfeat(0)
             if i == 1:
-                quantise_tfeat()
+                quantise_tfeat(1)
             if is_tile(u_t):
                 quantise_u(u_t)
             if is_tile(e_t):

@@ -37,6 +37,7 @@ W_TILES_PER_HALF = W_TILES // HALVES
 W_ROUNDS = ((), (0, 1), (2, 3), (4, 5), (6,), (7,))
 W_QUANTISE_ROUNDS = (3, 4, 6)
 LAST_WIDTH = 256
+V_TILES = (0,)
 WARM_MATMULS = 4
 TF_PIECE = 256
 RIDERS = 2
@@ -72,12 +73,13 @@ def tile_reins_attention4_pa_kernel(tc, body, tokens, tfeat, Wf, b_f, scale, out
         for a in range(TOKENS // P):
             nc.sync.dma_start(out=tok_sb[:, a, :], in_=tok_rows[:, a, :])
         nc.sync.dma_start(out=x_pairs[0][:, 1, :], in_=x_rows[:, 1, :])
+        nc.sync.dma_start(out=x_pairs[1][:, 0, :], in_=x_rows[:, 2, :])
         nc.sync.dma_start(
             out=tf_raw[:].rearrange("q (h e) c -> q h (e c)", e=2),
             in_=tfeat.rearrange("(h q e) c -> q h (e c)", h=2, e=2),
         )
-        load_x(1)
         load_w(0)
+        nc.sync.dma_start(out=x_pairs[1][:, 1, :], in_=x_rows[:, 3, :])
         load_w(1)
         load_x(2)
         load_w(2)
@@ -131,6 +133,10 @@ def tile_reins_attention4_pa_kernel(tc, body, tokens, tfeat, Wf, b_f, scale, out
                 nc.gpsimd.tensor_tensor(
                     out=residual[t][:, cols], in0=x_tile(t)[:, cols], in1=scaled_bias[:, cols], op=ALU.add
                 )
+
+        def v_residual(t, h):
+            cols = slice(h * BANK, (h + 1) * BANK)
+            nc.vector.tensor_tensor(out=residual[t][:, cols], in0=x_tile(t)[:, cols], in1=scaled_bias[:, cols], op=ALU.add)
 
         def turn_bank(blocks, name):
             return banks.tile([P, blocks, P], F32, tag="bank", name=name)
@@ -224,7 +230,7 @@ def tile_reins_attention4_pa_kernel(tc, body, tokens, tfeat, Wf, b_f, scale, out
         score_half(1)
         for h in range(HALVES):
             scale_bias(h)
-        for t in range(ROW_TILES):
+        for t in [t for t in range(ROW_TILES) if t not in V_TILES]:
             prepare_residual(t)
 
         tf_grouped = keep.tile([P, FEAT, PACK], BF16, name="tf_grouped", align_bytes=64)
@@ -424,6 +430,8 @@ def tile_reins_attention4_pa_kernel(tc, body, tokens, tfeat, Wf, b_f, scale, out
                 empty_u_bank(u_t, u_bank)
             if is_tile(e_t):
                 empty_e_bank(e_t, e_bank)
+            if i == 0:
+                group_tfeat(nc.scalar.copy, 1)
             if is_tile(i):
                 softmax_numerators(i, score_bank)
 
@@ -431,7 +439,6 @@ def tile_reins_attention4_pa_kernel(tc, body, tokens, tfeat, Wf, b_f, scale, out
                 group_tfeat(nc.vector.tensor_copy, 0)
                 group_tfeat(nc.vector.tensor_copy, 2)
                 group_tfeat(nc.vector.tensor_copy, 3)
-                group_tfeat(nc.scalar.copy, 1)
                 quantise_tfeat(0)
             if i == 1:
                 quantise_tfeat(1)
@@ -440,6 +447,10 @@ def tile_reins_attention4_pa_kernel(tc, body, tokens, tfeat, Wf, b_f, scale, out
             if is_tile(e_t):
                 quantise_e(e_t)
 
+            if i == 1:
+                for t in V_TILES:
+                    for h in range(HALVES):
+                        v_residual(t, h)
             if is_tile(i - ATTEND_LAG):
                 attend(i - ATTEND_LAG)
             if is_tile(i - PROJECT_LAG):

@@ -40,7 +40,6 @@ LAST_WIDTH = 256
 V_TILES = (0,)
 WARM_MATMULS = 4
 TF_PIECE = 256
-RIDERS = 2
 
 FLOPS = 2 * ROWS * FEAT * TOKENS + 2 * ROWS * TOKENS * FEAT + 2 * ROWS * FEAT * FEAT
 
@@ -184,8 +183,8 @@ def tile_reins_attention4_pa_kernel(tc, body, tokens, tfeat, Wf, b_f, scale, out
             for k in range(SCORE_PASSES):
                 score_pass(0, score_bank, k, slice(h, h + 1))
 
-        def invert_sum(t):
-            col = slice(t, t + 1)
+        def invert_sums(t):
+            col = slice(t, t + 2)
             nc.vector.reciprocal(out=e_sum_inv[:, col], in_=e_sum[:, col])
 
         def softmax_numerators(t, bank):
@@ -400,15 +399,15 @@ def tile_reins_attention4_pa_kernel(tc, body, tokens, tfeat, Wf, b_f, scale, out
             if is_tile(i):
                 if i > 0:
                     score_bank = banks.tile([P, 2, 2 * P], F32, tag="bank", name="score_bank")
-                first_place = RIDERS * (SCORE_PASSES - 1) - len(turns)
-                assert first_place >= 0
+                spaces = SCORE_PASSES - 1
                 for k in range(SCORE_PASSES):
                     if i > 0:
                         score_pass(i, score_bank, k, slice(0, 2))
-                    for place in range(max(k * RIDERS, first_place), min(k + 1, SCORE_PASSES - 1) * RIDERS):
-                        turn(*turns[place - first_place])
-                if i > 0:
-                    invert_sum(i - 1)
+                    if k < spaces:
+                        for dst, src in turns[k * len(turns) // spaces : (k + 1) * len(turns) // spaces]:
+                            turn(dst, src)
+                if i > 0 and i % 2 == 0:
+                    invert_sums(i - 2)
                 nc.vector.tensor_reduce(
                     out=neg_max[:, i : i + 1],
                     in_=score_bank[:].rearrange("p a m -> p (a m)"),
@@ -454,7 +453,7 @@ def tile_reins_attention4_pa_kernel(tc, body, tokens, tfeat, Wf, b_f, scale, out
             if is_tile(i - ATTEND_LAG):
                 attend(i - ATTEND_LAG)
             if is_tile(i - PROJECT_LAG):
-                project(i - PROJECT_LAG)
+                (project if i - PROJECT_LAG in (0, 1, 2, 3, 4, 6,) else project_beside_none)(i - PROJECT_LAG)
 
         def turn_u(t):
             bank = turn_bank(FEAT_BLOCKS, "u_bank")
@@ -468,7 +467,7 @@ def tile_reins_attention4_pa_kernel(tc, body, tokens, tfeat, Wf, b_f, scale, out
                 turn(dst, src)
             empty_e_bank(t, bank)
 
-        invert_sum(7)
+        invert_sums(6)
         attend(6)
         project(2)
         turn_e(7)
@@ -485,5 +484,5 @@ def tile_reins_attention4_pa_kernel(tc, body, tokens, tfeat, Wf, b_f, scale, out
         project_beside_none(5)
         turn_u(7)
         quantise_u(7)
-        project_beside_none(6)
+        project(6)
         project_last(7)

from contextlib import ExitStack

import concourse.mybir as mybir
from concourse.masks import make_identity

F32 = mybir.dt.float32
BF16 = mybir.dt.bfloat16
U32 = mybir.dt.uint32
U8 = mybir.dt.uint8
FP8X4 = mybir.dt.float8_e4m3fn_x4
ALU = mybir.AluOpType
ACT = mybir.ActivationFunctionType
AXIS = mybir.AxisListType

P = 128
ROWS = 1024
FEAT = 1024
TOKENS = 512
BANK = 512
PACK = 4
WORDS = FEAT // 2
ROW_TILES = ROWS // P
FEAT_BLOCKS = WORDS // P
FEAT_PASSES = FEAT // (P * PACK)
HALVES = FEAT // BANK
SCORE_SCALE = FEAT ** -0.5
SCORE_PASSES = FEAT // P

X_LEAD = 1
E_LAG = 1
ATTEND_LAG = 2
U_LAG = 4
PROJECT_LAG = 6
ROUNDS = ROW_TILES + PROJECT_LAG
W_TILES = FEAT // P
W_TILES_PER_HALF = W_TILES // HALVES
W_ROUNDS = ((), (0, 1), (2, 3), (4, 5), (6,), (7,))
W_QUANTISE_ROUNDS = (3, 4, 6)
LAST_WIDTH = 256
V_TILES = (0,)
WARM_MATMULS = 4
TF_PIECE = 256

FLOPS = 2 * ROWS * FEAT * TOKENS + 2 * ROWS * TOKENS * FEAT + 2 * ROWS * FEAT * FEAT


def tile_reins_attention4_pa_kernel(tc, body, tokens, tfeat, Wf, b_f, scale, out):
    nc = tc.nc
    x_rows = body.flatten_outer_dims().rearrange("(p t) c -> p t c", t=ROW_TILES)
    out_rows = out.flatten_outer_dims().rearrange("(p t) c -> p t c", t=ROW_TILES)

    with ExitStack() as ctx:
        ctx.enter_context(tc.manual_schedule())
        keep = ctx.enter_context(tc.tile_pool(name="keep", bufs=1))
        ring = ctx.enter_context(tc.tile_pool(name="ring", bufs=3))
        banks = ctx.enter_context(tc.psum_pool(name="banks", bufs=8))

        x_pairs = [keep.tile([P, 2, FEAT], BF16, name="x_pair%d" % j) for j in range(ROW_TILES // 2)]
        w_pairs = [keep.tile([P, 2, FEAT], BF16, name="w_pair%d" % j) for j in range(FEAT // P // 2)]
        tok_sb = keep.tile([P, TOKENS // P, FEAT], BF16, name="tok_sb")
        tf_raw = keep.tile([P, PACK, FEAT], BF16, name="tf_raw")
        tok_rows = tokens.rearrange("(a p) c -> p a c", p=P)
        w_rows = Wf.rearrange("(a p) c -> p a c", p=P)

        def load_x(j):
            nc.sync.dma_start(out=x_pairs[j][:], in_=x_rows[:, 2 * j : 2 * j + 2, :])

        def load_w(j):
            nc.sync.dma_start(out=w_pairs[j][:], in_=w_rows[:, 2 * j : 2 * j + 2, :])

        nc.sync.dma_start(out=x_pairs[0][:, 0, :], in_=x_rows[:, 0, :])
        for a in range(TOKENS // P):
            nc.sync.dma_start(out=tok_sb[:, a, :], in_=tok_rows[:, a, :])
        nc.sync.dma_start(out=x_pairs[0][:, 1, :], in_=x_rows[:, 1, :])
        nc.sync.dma_start(out=x_pairs[1][:, 0, :], in_=x_rows[:, 2, :])
        nc.sync.dma_start(
            out=tf_raw[:].rearrange("q (h e) c -> q h (e c)", e=2),
            in_=tfeat.rearrange("(h q e) c -> q h (e c)", h=2, e=2),
        )
        load_w(0)
        nc.sync.dma_start(out=x_pairs[1][:, 1, :], in_=x_rows[:, 3, :])
        load_w(1)
        load_x(2)
        load_w(2)
        load_x(3)
        load_w(3)

        def x_tile(t):
            return x_pairs[t // 2][:, t % 2, :]

        def w_tile(a):
            return w_pairs[a // 2][:, a % 2, :]

        ident = keep.tile([P, P], F32, name="ident")
        make_identity(nc, ident[:])

        SPARE = 32
        row0 = keep.tile([P, FEAT + SPARE], BF16, name="row0")
        nc.vector.memset(row0[:].bitcast(U32), 0)
        ones = keep.tile([P, BANK], BF16, name="ones")
        nc.vector.memset(ones[:], 1.0)
        nc.scalar.dma_start(out=row0[0:1, 0:FEAT], in_=b_f.unsqueeze(0))
        nc.scalar.dma_start(out=row0[0:1, FEAT : FEAT + 1], in_=scale.unsqueeze(0))
        scale_col = keep.tile([P, 1], F32, name="scale_col")
        scaled_bias = keep.tile([P, FEAT], F32, name="scaled_bias")
        residual = [keep.tile([P, FEAT], F32, name="residual%d" % t) for t in range(ROW_TILES)]

        def spread_rows():
            scale_bank = banks.tile([P, SPARE], F32, tag="bank", name="scale_bank")
            nc.tensor.matmul(out=scale_bank[:], lhsT=ones[:, 0:P], rhs=row0[:, FEAT:], start=True, stop=True)
            nc.scalar.copy(out=scale_col[:], in_=scale_bank[:, 0:1])
            bias_banks = []
            for h in range(HALVES):
                bias_bank = banks.tile([P, BANK], F32, tag="bank", name="bias_bank%d" % h)
                bias_row = row0[:, h * BANK : (h + 1) * BANK]
                nc.tensor.matmul(out=bias_bank[:], lhsT=ones[:, 0:P], rhs=bias_row, start=True, stop=True)
                bias_banks.append(bias_bank)
            return bias_banks

        def scale_bias(h):
            cols = slice(h * BANK, (h + 1) * BANK)
            nc.scalar.activation(out=scaled_bias[:, cols], in_=bias_banks[h][:], func=ACT.Copy, scale=scale_col[:])

        def warm(n):
            warm_bank = banks.tile([P, BANK], F32, tag="bank", name="warm_bank")
            for j in range(n):
                nc.tensor.matmul(out=warm_bank[:], lhsT=ones[:, 0:P], rhs=ones[:], start=True, stop=True)

        def prepare_residual(t):
            for h in range(HALVES):
                cols = slice(h * BANK, (h + 1) * BANK)
                nc.gpsimd.tensor_tensor(
                    out=residual[t][:, cols], in0=x_tile(t)[:, cols], in1=scaled_bias[:, cols], op=ALU.add
                )

        def v_residual(t, h):
            cols = slice(h * BANK, (h + 1) * BANK)
            nc.vector.tensor_tensor(out=residual[t][:, cols], in0=x_tile(t)[:, cols], in1=scaled_bias[:, cols], op=ALU.add)

        def turn_bank(blocks, name):
            return banks.tile([P, blocks, P], F32, tag="bank", name=name)

        def turns_into(bank, rows_bf16, blocks):
            words = rows_bf16.bitcast(F32)
            return [(bank[:, b, :], words[:, b * P : (b + 1) * P]) for b in range(blocks)]

        def turn(dst, src):
            nc.tensor.transpose(out=dst, in_=src, identity=ident[:])

        def group_words(grouped, bank):
            nc.scalar.copy(
                out=grouped.bitcast(F32).rearrange("q g (r h) -> q g r h", h=2),
                in_=bank[:].rearrange("q (g h) r -> q g r h", h=2),
            )

        tok_T = keep.tile([P, 2, FEAT_BLOCKS, 2, 2 * P], BF16, name="tok_T")
        x_T = {}

        def turn_x_early(t):
            x_bank = turn_bank(FEAT_BLOCKS, "x_bank")
            for dst, src in turns_into(x_bank, x_tile(t), FEAT_BLOCKS):
                turn(dst, src)
            x_T[t] = ring.tile([P, FEAT_BLOCKS, P], F32, name="x_T", bufs=X_LEAD + 2)
            nc.vector.tensor_copy(out=x_T[t][:], in_=x_bank[:])

        neg_max = keep.tile([P, ROW_TILES], F32, name="neg_max")
        e_sum = keep.tile([P, ROW_TILES], F32, name="e_sum")
        e_sum_inv = keep.tile([P, ROW_TILES], F32, name="e_sum_inv")
        e_rows = {}

        def score_pass(t, bank, k, halves):
            block, e = k // 2, k % 2
            x_halves = x_T[t][:].bitcast(BF16).rearrange("q b (r e) -> q b r e", e=2)
            nc.tensor.matmul(
                out=bank[:, halves, :],
                lhsT=x_halves[:, block, :, e],
                rhs=tok_T[:, halves, block, e, :],
                start=(k == 0),
                stop=(k == SCORE_PASSES - 1),
            )

        def score_half(h):
            for k in range(SCORE_PASSES):
                score_pass(0, score_bank, k, slice(h, h + 1))

        def invert_sums(t):
            col = slice(t, t + 2)
            nc.vector.reciprocal(out=e_sum_inv[:, col], in_=e_sum[:, col])

        def softmax_numerators(t, bank):
            col = slice(t, t + 1)
            e_rows[t] = ring.tile([P, TOKENS], BF16, name="e_rows")
            nc.scalar.activation(
                out=e_rows[t][:],
                in_=bank[:].rearrange("p a m -> p (a m)"),
                func=ACT.Exp,
                bias=neg_max[:, col],
                accum_out=e_sum[:, col],
            )

        warm(WARM_MATMULS)
        turn_x_early(0)
        def turn_tokens(a):
            tok_words = tok_sb[:, a, :].bitcast(F32)
            cols = slice(a % 2 * P, (a % 2 + 1) * P)
            for half in range(2):
                blocks = slice(2 * half, 2 * half + 2)
                tok_bank = banks.tile([P, 2, P], F32, tag="bank", name="tok_bank")
                for j in range(2):
                    b = 2 * half + j
                    turn(tok_bank[:, j, :], tok_words[:, b * P : (b + 1) * P])
                halves = tok_bank[:].rearrange("q b m -> q (b m)").bitcast(BF16)
                halves = halves.rearrange("q (b m e) -> q b e m", b=2, e=2)
                if half == 0:
                    nc.vector.tensor_scalar(
                        out=tok_T[:, a // 2, blocks, :, cols], in0=halves, scalar1=SCORE_SCALE, scalar2=None, op0=ALU.mult
                    )
                else:
                    nc.scalar.activation(
                        out=tok_T[:, a // 2, blocks, :, cols], in_=halves, func=ACT.Copy, scale=SCORE_SCALE
                    )

        score_bank = banks.tile([P, 2, 2 * P], F32, tag="bank", name="score_bank")
        for a in range(TOKENS // P):
            turn_tokens(a)
        bias_banks = spread_rows()
        score_half(0)
        turn_x_early(1)
        score_half(1)
        for h in range(HALVES):
            scale_bias(h)
        for t in [t for t in range(ROW_TILES) if t not in V_TILES]:
            prepare_residual(t)

        tf_grouped = keep.tile([P, FEAT, PACK], BF16, name="tf_grouped", align_bytes=64)
        tf_codes = keep.tile([P, FEAT], U32, name="tf_codes", align_bytes=64)
        tf_scales = keep.tile([P, FEAT], U8, name="tf_scales", align_bytes=64)

        def group_tfeat(copy, piece):
            cols = slice(piece * TF_PIECE, (piece + 1) * TF_PIECE)
            copy(
                out=tf_grouped[:, cols, :].rearrange("q (c i) j -> q c j i", i=4),
                in_=tf_raw[:, :, cols].rearrange("q j (c i) -> q c j i", i=4),
            )

        def quantise_tfeat(h):
            cols = slice(h * BANK, (h + 1) * BANK)
            nc.vector.quantize_mx(
                out=tf_codes[:, cols].bitcast(FP8X4),
                scales=tf_scales[:, cols],
                in_=tf_grouped[:, cols, :].rearrange("q c j -> q (c j)"),
            )

        e_codes = {}
        e_scales = {}
        u_rows = {}

        def attend(t):
            col = slice(t, t + 1)
            u_rows[t] = ring.tile([P, FEAT], BF16, name="u_rows", bufs=U_LAG - ATTEND_LAG + 2)
            for h in range(HALVES):
                cols = slice(h * BANK, (h + 1) * BANK)
                bank = banks.tile([P, BANK], F32, tag="bank", name="delta_bank")
                nc.tensor.matmul_mx(
                    out=bank[:],
                    lhsT=e_codes[t][:].bitcast(FP8X4),
                    lhsT_scale=e_scales[t][:],
                    rhs=tf_codes[:, cols].bitcast(FP8X4),
                    rhs_scale=tf_scales[:, cols],
                    start=True,
                    stop=True,
                )
                nc.vector.scalar_tensor_tensor(
                    out=u_rows[t][:, cols],
                    in0=bank[:],
                    scalar=e_sum_inv[:, col],
                    in1=x_tile(t)[:, cols],
                    op0=ALU.mult,
                    op1=ALU.add,
                )

        w_codes = keep.tile([P, FEAT_PASSES, FEAT], U32, name="w_codes", align_bytes=64)
        w_scales = keep.tile([P, FEAT_PASSES, FEAT], U8, name="w_scales", align_bytes=64)
        w_grouped = [
            keep.tile([P, FEAT_PASSES, BANK * PACK], BF16, name="w_grouped%d" % h, align_bytes=64) for h in range(HALVES)
        ]
        u_codes = [keep.tile([P, FEAT_PASSES, P], U32, name="u_codes%d" % t, align_bytes=64) for t in range(ROW_TILES)]
        u_scales = [keep.tile([P, FEAT_PASSES, P], U8, name="u_scales%d" % t, align_bytes=64) for t in range(ROW_TILES)]

        def w_quantise(h, g):
            rows = slice(h * BANK, (h + 1) * BANK)
            nc.vector.quantize_mx(
                out=w_codes[:, g, rows].bitcast(FP8X4), scales=w_scales[:, g, rows], in_=w_grouped[h][:, g, :]
            )

        def project_passes(t, first, width):
            cols = slice(first, first + width)
            bank = banks.tile([P, width], F32, tag="bank", name="y_bank")
            for g in range(FEAT_PASSES):
                nc.tensor.matmul_mx(
                    out=bank[:],
                    lhsT=u_codes[t][:, g, :].bitcast(FP8X4),
                    lhsT_scale=u_scales[t][:, g, :],
                    rhs=w_codes[:, g, cols].bitcast(FP8X4),
                    rhs_scale=w_scales[:, g, cols],
                    start=(g == 0),
                    stop=(g == FEAT_PASSES - 1),
                )
            return bank

        def finish_on_vector(t, first, width, bank, queue):
            cols = slice(first, first + width)
            result = ring.tile([P, BANK], F32, name="result", bufs=8)
            nc.vector.scalar_tensor_tensor(
                out=result[:, 0:width],
                in0=bank[:],
                scalar=scale_col[:],
                in1=residual[t][:, cols],
                op0=ALU.mult,
                op1=ALU.add,
            )
            queue.dma_start(out=out_rows[:, t, cols], in_=result[:, 0:width])

        def finish_beside_vector(t, first, width, bank):
            cols = slice(first, first + width)
            scaled = ring.tile([P, width], F32, name="scaled")
            nc.scalar.activation(out=scaled[:], in_=bank[:], func=ACT.Copy, scale=scale_col[:])
            result = ring.tile([P, width], F32, name="result_beside", bufs=6)
            nc.gpsimd.tensor_tensor(out=result[:], in0=scaled[:], in1=residual[t][:, cols], op=ALU.add)
            nc.sync.dma_start(out=out_rows[:, t, cols], in_=result[:])

        def project_banks(t):
            return [project_passes(t, h * BANK, BANK) for h in range(HALVES)]

        def finish(t, y_banks):
            finish_on_vector(t, BANK, BANK, y_banks[1], nc.sync)
            finish_beside_vector(t, 0, BANK, y_banks[0])

        def project(t):
            finish(t, project_banks(t))

        def project_beside_none(t):
            y_banks = project_banks(t)
            for h in range(HALVES):
                finish_on_vector(t, h * BANK, BANK, y_banks[h], nc.sync)

        def project_last(t):
            for first in range(0, FEAT, LAST_WIDTH):
                finish_on_vector(t, first, LAST_WIDTH, project_passes(t, first, LAST_WIDTH), nc.scalar)

        def is_tile(t):
            return 0 <= t < ROW_TILES

        def empty_u_bank(t, bank):
            u_grouped[t] = ring.tile([P, FEAT_PASSES, P * PACK], BF16, name="u_grouped", align_bytes=256)
            group_words(u_grouped[t][:], bank)

        def empty_e_bank(t, bank):
            e_grouped[t] = ring.tile([P, 1, P * PACK], BF16, name="e_grouped", align_bytes=256)
            group_words(e_grouped[t][:], bank)

        u_grouped = {}
        e_grouped = {}

        def quantise_u(t):
            nc.vector.quantize_mx(
                out=u_codes[t][:].rearrange("q g r -> q (g r)").bitcast(FP8X4),
                scales=u_scales[t][:].rearrange("q g r -> q (g r)"),
                in_=u_grouped[t][:].rearrange("q g c -> q (g c)"),
            )

        def quantise_e(t):
            e_codes[t] = ring.tile([P, P], U32, name="e_codes", align_bytes=256)
            e_scales[t] = ring.tile([P, P], U8, name="e_scales", align_bytes=256)
            nc.vector.quantize_mx(out=e_codes[t][:].bitcast(FP8X4), scales=e_scales[t][:], in_=e_grouped[t][:, 0, :])

        for i in range(ROW_TILES):
            u_t, e_t = i - U_LAG, i - E_LAG
            x_now = [t for t in [i + X_LEAD] if 2 <= t < ROW_TILES]
            w_now = W_ROUNDS[i] if i < len(W_ROUNDS) else ()
            if i in W_QUANTISE_ROUNDS:
                w_quantise(*divmod(W_QUANTISE_ROUNDS.index(i), FEAT_PASSES))
                if i == W_QUANTISE_ROUNDS[-1]:
                    w_quantise(1, 1)

            turns = []
            x_banks = [turn_bank(FEAT_BLOCKS, "x_bank") for t in x_now]
            for t, x_bank in zip(x_now, x_banks):
                turns.extend(turns_into(x_bank, x_tile(t), FEAT_BLOCKS))
            w_banks = [turn_bank(FEAT_BLOCKS, "w_bank") for a in w_now]
            for a, w_bank in zip(w_now, w_banks):
                turns.extend(turns_into(w_bank, w_tile(a), FEAT_BLOCKS))
            if is_tile(u_t):
                u_bank = turn_bank(FEAT_BLOCKS, "u_bank")
                turns.extend(turns_into(u_bank, u_rows[u_t][:], FEAT_BLOCKS))
            if is_tile(e_t):
                e_bank = turn_bank(TOKENS // 2 // P, "e_bank")
                turns.extend(turns_into(e_bank, e_rows[e_t][:], TOKENS // 2 // P))
            if is_tile(i):
                if i > 0:
                    score_bank = banks.tile([P, 2, 2 * P], F32, tag="bank", name="score_bank")
                spaces = SCORE_PASSES - 1
                for k in range(SCORE_PASSES):
                    if i > 0:
                        score_pass(i, score_bank, k, slice(0, 2))
                    if k < spaces:
                        for dst, src in turns[k * len(turns) // spaces : (k + 1) * len(turns) // spaces]:
                            turn(dst, src)
                if i > 0 and i % 2 == 0:
                    invert_sums(i - 2)
                nc.vector.tensor_reduce(
                    out=neg_max[:, i : i + 1],
                    in_=score_bank[:].rearrange("p a m -> p (a m)"),
                    axis=AXIS.X,
                    op=ALU.max,
                    negate=True,
                )
            else:
                for dst, src in turns:
                    turn(dst, src)

            for t, x_bank in zip(x_now, x_banks):
                x_T[t] = ring.tile([P, FEAT_BLOCKS, P], F32, name="x_T", bufs=X_LEAD + 2)
                nc.scalar.copy(out=x_T[t][:], in_=x_bank[:])
            for a, w_bank in zip(w_now, w_banks):
                h, rows = a // W_TILES_PER_HALF, slice(a % W_TILES_PER_HALF * P * PACK, (a % W_TILES_PER_HALF + 1) * P * PACK)
                group_words(w_grouped[h][:, :, rows], w_bank)
            if is_tile(u_t):
                empty_u_bank(u_t, u_bank)
            if is_tile(e_t):
                empty_e_bank(e_t, e_bank)
            if i == 0:
                group_tfeat(nc.scalar.copy, 1)
            if is_tile(i):
                softmax_numerators(i, score_bank)

            if i == 0:
                group_tfeat(nc.vector.tensor_copy, 0)
                group_tfeat(nc.vector.tensor_copy, 2)
                group_tfeat(nc.vector.tensor_copy, 3)
                quantise_tfeat(0)
            if i == 1:
                quantise_tfeat(1)
            if is_tile(u_t):
                quantise_u(u_t)
            if is_tile(e_t):
                quantise_e(e_t)

            if i == 1:
                for t in V_TILES:
                    for h in range(HALVES):
                        v_residual(t, h)
            if is_tile(i - ATTEND_LAG):
                attend(i - ATTEND_LAG)
            if is_tile(i - PROJECT_LAG):
                (project if i - PROJECT_LAG in (0, 1, 2, 3, 4, 6,) else project_beside_none)(i - PROJECT_LAG)

        def turn_u(t):
            bank = turn_bank(FEAT_BLOCKS, "u_bank")
            for dst, src in turns_into(bank, u_rows[t][:], FEAT_BLOCKS):
                turn(dst, src)
            empty_u_bank(t, bank)

        def turn_e(t):
            bank = turn_bank(TOKENS // 2 // P, "e_bank")
            for dst, src in turns_into(bank, e_rows[t][:], TOKENS // 2 // P):
                turn(dst, src)
            empty_e_bank(t, bank)

        invert_sums(6)
        attend(6)
        project(2)
        turn_e(7)
        turn_u(4)
        turn_u(5)
        turn_u(6)
        quantise_e(7)
        quantise_u(4)
        quantise_u(5)
        project(3)
        attend(7)
        quantise_u(6)
        project(4)
        project_beside_none(5)
        turn_u(7)
        quantise_u(7)
        project(6)
        project_last(7)
